import numpy as np
import ml_dtypes


def mxq(x, axis, fmt="e4m3"):
    dtype, down = {"e4m3": (ml_dtypes.float8_e4m3fn, 7), "e5m2": (ml_dtypes.float8_e5m2, 14)}[fmt]
    v = np.moveaxis(np.asarray(x, np.float32).astype(ml_dtypes.bfloat16).astype(np.float64), axis, -1)
    blocks = v.reshape(v.shape[:-1] + (-1, 32))
    amax = np.abs(blocks).max(-1, keepdims=True)
    byte = np.maximum(np.where(amax > 0, np.frexp(amax)[1] - 1 + 127, 0) - down, 1)
    scale = np.exp2(byte - 127.0)
    codes = (blocks / scale).astype(np.float32).astype(dtype).astype(np.float64)
    return np.moveaxis((codes * scale).reshape(v.shape), -1, axis)


WIDE = False


def mx_kscale(k):
    if not WIDE:
        return np.ones(k)
    levels = np.array([18, -18])
    if k % 512:
        return np.exp2(np.random.permutation(np.resize(levels, k // 32))).repeat(32)
    a = np.empty((k // 512, 16))
    for p in range(k // 512):
        a[p, :8] = np.random.permutation(np.resize(levels, 8))
        for g in range(8):
            far = levels[np.abs(levels - a[p, g]) >= 10]
            a[p, g + 8] = far[np.random.randint(len(far))]
    return np.exp2(a.ravel()).repeat(32)


BF16 = ml_dtypes.bfloat16


def bf(x):
    return np.asarray(x, np.float32).astype(BF16)


def f64(x):
    return np.asarray(x).astype(np.float64)


B, S, H, NH, NKV, HD = 2, 512, 1024, 8, 4, 128
ROPE_THETA = 10000.0


def rope_tables():
    inv_freq = 1.0 / (ROPE_THETA ** (np.arange(0, HD, 2) / HD))
    pos = np.arange(S)[None, :] + np.random.randint(0, S, (B, 1))
    freqs = pos[:, :, None] * inv_freq[None, None, :]
    emb = np.concatenate([freqs, freqs], axis=-1)
    return np.cos(emb), np.sin(emb)


def rotate_half(x):
    x1, x2 = np.split(x, 2, axis=-1)
    return np.concatenate([-x2, x1], axis=-1)


def rotate_half_back(a):
    a1, a2 = np.split(a, 2, axis=-1)
    return np.concatenate([a2, -a1], axis=-1)


def merge_heads(a):
    b, n, s, d = a.shape
    return a.transpose(0, 2, 1, 3).reshape(b * s, n * d)


def setup_inputs():
    s = mx_kscale(B * S).reshape(B, S)
    half = mx_kscale((NH + 2 * NKV) * (HD // 2)).reshape(NH + 2 * NKV, HD // 2)
    u = np.concatenate([half, half], axis=1)
    uq, uk, uv = u[:NH], u[NH:NH + NKV], u[NH + NKV:]
    hidden_states = bf(np.random.standard_normal((B, S, H)) * s[:, :, None])
    q_w = bf(np.random.standard_normal((NH * HD, H)) / np.sqrt(H) / uq.reshape(-1)[:, None])
    k_w = bf(np.random.standard_normal((NKV * HD, H)) / np.sqrt(H) / uk.reshape(-1)[:, None])
    v_w = bf(np.random.standard_normal((NKV * HD, H)) / np.sqrt(H) / uv.reshape(-1)[:, None])
    cos, sin = rope_tables()
    e = np.exp2(np.random.randint(-6, 1, (B, 1, S, 1)))
    st = s[:, None, :, None]
    grad_0 = bf(np.random.standard_normal((B, NH, S, HD)) * e / st * uq[None, :, None, :])
    grad_1 = bf(np.random.standard_normal((B, NKV, S, HD)) * e / st * uk[None, :, None, :])
    grad_2 = bf(np.random.standard_normal((B, NKV, S, HD)) * e / st * uv[None, :, None, :])
    return {"hidden_states": hidden_states, "cos": bf(cos), "sin": bf(sin), "q_w": q_w, "k_w": k_w, "v_w": v_w,
            "grad_0": grad_0, "grad_1": grad_1, "grad_2": grad_2}


def reference(hidden_states, cos, sin, q_w, k_w, v_w, grad_0, grad_1, grad_2):
    b, s, h = hidden_states.shape
    x = f64(hidden_states).reshape(b * s, h)
    c = f64(cos)[:, None, :, :]
    sn = f64(sin)[:, None, :, :]
    g0, g1, g2 = f64(grad_0), f64(grad_1), f64(grad_2)
    dq = merge_heads(g0 * c + rotate_half_back(g0 * sn))
    dk = merge_heads(g1 * c + rotate_half_back(g1 * sn))
    dv = merge_heads(g2)
    dz = np.concatenate([dq, dk, dv], axis=1)
    w = np.concatenate([f64(q_w), f64(k_w), f64(v_w)], axis=0)
    dx = mxq(dz, 1, "e5m2") @ mxq(w, 0, "e4m3")
    dw = mxq(dq, 0, "e5m2").T @ mxq(x, 0, "e4m3")
    return dx.reshape(b, s, h), dw

@@ -1,0 +1,411 @@
+from contextlib import ExitStack
+
+import concourse.mybir as mybir
+from concourse.masks import make_identity
+
+B, S, H, HD = 2, 512, 1024, 128
+FLOPS = 2 * 1024 * 2048 * 1024 + 2 * 1024 * 1024 * 1024
+
+F32 = mybir.dt.float32
+BF16 = mybir.dt.bfloat16
+U32 = mybir.dt.uint32
+U8 = mybir.dt.uint8
+E4 = mybir.dt.float8_e4m3fn_x4
+E5 = mybir.dt.float8_e5m2_x4
+MULT = mybir.AluOpType.mult
+ADD = mybir.AluOpType.add
+P = 128
+
+
+def tile_mistralattention_v_kernel(tc, hidden_states, cos, sin, q_w, k_w, v_w, grad_0, grad_1, grad_2, out_0, out_1):
+    nc = tc.nc
+    with ExitStack() as ctx:
+        keep = ctx.enter_context(tc.tile_pool(name="keep", bufs=1))
+        work = ctx.enter_context(tc.tile_pool(name="work", bufs=2))
+        psum = ctx.enter_context(tc.psum_pool(name="psum", bufs=1))
+        ctx.enter_context(tc.manual_schedule())
+
+        def kept(shape, dtype, name):
+            return keep.tile(shape, dtype, name=name, align_bytes=64)
+
+        tab = [kept([P, 2, 512], BF16, "tab%d" % b) for b in range(B)]
+        sin_raw = [kept([P, 4, 2, 64], BF16, "sin%d" % b) for b in range(B)]
+        g_a = [kept([P, 4, 512], BF16, "ga%d" % b) for b in range(B)]
+        g_q = [kept([P, 4, 512], BF16, "gq%d" % b) for b in range(B)]
+        g_k = [kept([P, 4, 512], BF16, "gk%d" % b) for b in range(B)]
+        g_v = [kept([P, 4, 512], BF16, "gv%d" % b) for b in range(B)]
+        w_raw = [work.tile([P, 4, H], BF16, name="wraw%d" % s, tag="raw", bufs=4) for s in range(4)]
+        x_raw = []
+        w_codes = [kept([P, H], U32, "wc%d" % s) for s in range(4)]
+        w_scales = [kept([P, H], U8, "ws%d" % s) for s in range(4)]
+        x_codes = [kept([P, H], U32, "xc%d" % b) for b in range(B)]
+        x_scales = [kept([P, H], U8, "xs%d" % b) for b in range(B)]
+        d_codes = [[kept([P, 512], U32, "dc%d%d" % (b, g)) for g in range(2)] for b in range(B)]
+        d_scales = [[kept([P, 512], U8, "ds%d%d" % (b, g)) for g in range(2)] for b in range(B)]
+        ident = kept([P, P], F32, "ident")
+
+        def heads(grad, b, h0):
+            return grad[b, h0:h0 + 4].rearrange("h (p j) d -> p h (j d)", j=4)
+
+        def load_tables(b):
+            nc.sync.dma_start(out=tab[b][:, 0, :], in_=cos[b].rearrange("(p j) d -> p (j d)", j=4))
+            nc.sync.dma_start(out=sin_raw[b][:].rearrange("p j a i -> p (j a i)"), in_=sin[b].rearrange("(p j) d -> p (j d)", j=4))
+
+        w_rows = [q_w[0:512, :], q_w[512:1024, :], v_w, k_w]
+
+        def load_w(s):
+            nc.sync.dma_start(out=w_raw[s][:], in_=w_rows[s].rearrange("(p j) h -> p j h", j=4))
+
+        def load_x(b):
+            x_raw.append(work.tile([P, 4, H], BF16, name="xraw%d" % b, tag="raw", bufs=4))
+            nc.sync.dma_start(out=x_raw[b][:], in_=hidden_states[b].rearrange("(p j) h -> p j h", j=4))
+
+        load_tables(0)
+        nc.sync.dma_start(out=g_a[0][:], in_=heads(grad_0, 0, 0))
+        load_w(0)
+        load_w(1)
+        nc.sync.dma_start(out=g_q[0][:], in_=heads(grad_0, 0, 4))
+        nc.sync.dma_start(out=g_k[0][:], in_=heads(grad_1, 0, 0))
+        load_w(3)
+        nc.sync.dma_start(out=g_v[0][:], in_=heads(grad_2, 0, 0))
+        load_w(2)
+        make_identity(nc, ident[:])
+
+        def turn_bank():
+            return psum.tile([P, 4, P], F32, name="turn", tag="turn", bufs=3)
+
+        def sum_bank():
+            return psum.tile([P, 512], F32, name="sums", tag="sums", bufs=4)
+
+        st = {}
+
+        def negate(b):
+            dst = tab[b][:, 1, :].rearrange("p (j a i) -> p j a i", j=4, a=2)
+            nc.vector.tensor_copy(out=dst[:, :, 0, :], in_=sin_raw[b][:, :, 1, :])
+            nc.vector.tensor_scalar(out=dst[:, :, 1, :], in0=sin_raw[b][:, :, 0, :], scalar1=-1.0, scalar2=None, op0=MULT)
+
+        def table_turn(b):
+            bank = turn_bank()
+            words = tab[b][:].rearrange("p s c -> p (s c)").bitcast(F32)
+            for c in range(4):
+                nc.tensor.transpose(bank[:, c, :], words[:, c * P:(c + 1) * P], ident[:])
+            turned = work.tile([P, 4, P], F32, name="tabT", tag="tabT", bufs=1)
+            nc.scalar.copy(out=turned[:], in_=bank[:])
+            st["tabT", b] = turned
+
+        def table_back(b):
+            bank = psum.tile([P, 4, P], F32, name="table", tag="table", bufs=1)
+            for c in range(4):
+                nc.tensor.transpose(bank[:, c, :], st["tabT", b][:, c, :], ident[:])
+            st["table", b] = bank[:].rearrange("p c w -> p (c w)").bitcast(BF16)
+
+        def products(b, s, j, from_sbuf=False):
+            g = g_a[b][:] if s == 0 else g_k[b][:]
+            table = tab[b][:].rearrange("p s c -> p (s c)") if from_sbuf else st["table", b]
+            table = table.rearrange("p (s j m t) -> p s j t m", s=2, j=4, t=4)
+            gv = g.rearrange("p h (j m t) -> p j t h m", j=4, t=4)[:, j]
+            t1 = work.tile([P, 4, 4, 32], F32, name="t1", tag="t1", bufs=3)
+            t2 = work.tile([P, 4, 4, 32], F32, name="t2", tag="t2", bufs=3)
+            nc.vector.tensor_tensor(out=t1[:], in0=gv, in1=table[:, 0, j].unsqueeze(2).to_broadcast([P, 4, 4, 32]), op=MULT)
+            for half in range(2):
+                src = slice(16 * (1 - half), 16 * (2 - half))
+                dst = slice(16 * half, 16 * (half + 1))
+                nc.vector.tensor_tensor(out=t2[:, :, :, dst], in0=gv[:, :, :, src],
+                                        in1=table[:, 1, j, :, dst].unsqueeze(2).to_broadcast([P, 4, 4, 16]), op=MULT)
+            st["t", b, s, j] = (t1, t2)
+
+        def products_q(b, j, part):
+            table = st["table", b].rearrange("p (s j a i) -> p s j a i", s=2, j=4, a=2)
+            gv = g_q[b][:].rearrange("p h (j a i) -> p j h a i", j=4, a=2)[:, j]
+            u = work.tile([P, 4, 2, 64], F32, name="u%d" % part, tag="u%d" % part, bufs=2)
+            nc.vector.tensor_tensor(out=u[:], in0=gv[:, :, ::-1, :] if part else gv,
+                                    in1=table[:, part, j].unsqueeze(1).to_broadcast([P, 4, 2, 64]), op=MULT)
+            st["u", part] = u
+            if part == 1:
+                if j == 0:
+                    st["dq", b] = work.tile([P, 4, 512], BF16, name="dq", tag="dq", bufs=2)
+                nc.gpsimd.tensor_tensor(out=st["dq", b][:, j, :], in0=st["u", 0][:].rearrange("p h a i -> p (h a i)"),
+                                        in1=u[:].rearrange("p h a i -> p (h a i)"), op=ADD)
+
+        def turn_words(b, j, engine):
+            bank = turn_bank()
+            for u in range(2):
+                nc.tensor.transpose(bank[:, 2 + u, :], st["vs", b][:, j, u, :], ident[:])
+            for u in range(2):
+                nc.tensor.transpose(bank[:, u, :], st["dq", b][:, j, :].bitcast(F32)[:, u:256:2], ident[:])
+            z = z_tile(b, j)
+            dst = z[:, 1:3, :].bitcast(F32).rearrange("p s (c u) -> p s c u", u=2)
+            src = bank[:].rearrange("p (s u) c -> p s c u", u=2)
+            if engine == "scalar":
+                nc.scalar.copy(out=dst, in_=src)
+            else:
+                nc.vector.tensor_copy(out=dst, in_=src)
+
+        def d_interleave(b, engine, c0, c1):
+            if c0 == 0:
+                st["d", b, 1] = work.tile([P, 512, 4], BF16, name="d", tag="d", bufs=2, align_bytes=64)
+            src = st["dq", b][:, :, c0:c1].rearrange("p j c -> p c j")
+            if engine == "scalar":
+                nc.scalar.copy(out=st["d", b, 1][:, c0:c1, :], in_=src)
+            else:
+                nc.vector.tensor_copy(out=st["d", b, 1][:, c0:c1, :], in_=src)
+
+        def z_tile(b, j):
+            if ("z", b, j) not in st:
+                st["z", b, j] = work.tile([P, 4, 512], BF16, name="z%d%d" % (b, j), tag="z", bufs=8, align_bytes=64)
+                st["zc", b, j] = work.tile([P, 4, P], U32, name="zc", tag="zc", bufs=6, align_bytes=64)
+                st["zs", b, j] = work.tile([P, 4, P], U8, name="zs", tag="zs", bufs=6, align_bytes=64)
+            return st["z", b, j]
+
+        def turn_sum(b, j, s):
+            t1, t2 = st["t", b, s, j]
+            bank = turn_bank()
+            for t in range(4):
+                for n, src in enumerate((t1, t2)):
+                    nc.tensor.matmul(bank[:, t, :], lhsT=src[:].rearrange("p t h m -> p t (h m)")[:, t, :], rhs=ident[:],
+                                     start=(n == 0), stop=(n == 1), is_transpose=True)
+            z = z_tile(b, j)
+            nc.scalar.copy(out=z[:, s, :].rearrange("p (c t) -> p c t", t=4), in_=bank[:].rearrange("p t c -> p c t"))
+
+        def sort_v(b):
+            vs = work.tile([P, 4, 2, P], F32, name="vs", tag="vs", bufs=1)
+            words = g_v[b][:].bitcast(F32).rearrange("p h (j m u) -> p j u h m", j=4, u=2)
+            for u in range(2):
+                nc.vector.tensor_copy(out=vs[:, :, u, :].rearrange("p j (h m) -> p j h m", h=4), in_=words[:, :, u])
+            st["vs", b] = vs
+
+        def quant_z(b, j, s0, s1):
+            nc.vector.quantize_mx(out=st["zc", b, j][:, s0:s1, :].rearrange("p s c -> p (s c)").bitcast(E5),
+                                  scales=st["zs", b, j][:, s0:s1, :].rearrange("p s c -> p (s c)"),
+                                  in_=st["z", b, j][:, s0:s1, :].rearrange("p s c -> p (s c)"))
+
+        def turn_back(b, u, engine):
+            if u == 0:
+                st["d", b, 0] = work.tile([P, 512, 4], BF16, name="d", tag="d", bufs=2, align_bytes=64)
+            bank = turn_bank()
+            for j in range(4):
+                nc.tensor.transpose(bank[:, j, :], st["z", b, j][:, 0, :].bitcast(F32)[:, u:256:2], ident[:])
+            dst = st["d", b, 0][:].rearrange("p (q u e) j -> p u q e j", u=2, e=2)[:, u]
+            src = bank[:].rearrange("p j q -> p (j q)").bitcast(BF16).rearrange("p (j q e) -> p q e j", j=4, e=2)
+            if engine == "scalar":
+                nc.scalar.copy(out=dst, in_=src)
+            else:
+                nc.vector.tensor_copy(out=dst, in_=src)
+
+        def quant_d(b, g):
+            nc.vector.quantize_mx(out=d_codes[b][g][:].bitcast(E5), scales=d_scales[b][g][:],
+                                  in_=st["d", b, g][:].rearrange("p c j -> p (c j)"))
+
+        def interleave(key, raw, share):
+            engine, c0, c1 = share
+            stage = work.tile([P, c1 - c0, 4], BF16, name="il" + engine, tag="il" + engine,
+                              bufs={"gpsimd": 1, "scalar": 3, "vector": 1}[engine], align_bytes=64)
+            src = raw[:, :, c0:c1].rearrange("p j c -> p c j")
+            if engine == "gpsimd":
+                nc.gpsimd.tensor_scalar(out=stage[:], in0=src, scalar1=1.0, scalar2=0.0, op0=MULT, op1=ADD)
+            elif engine == "scalar":
+                nc.scalar.copy(out=stage[:], in_=src)
+            else:
+                nc.vector.tensor_copy(out=stage[:], in_=src)
+            st["il", key, c0] = stage
+
+        def quant_rows(key, codes, scales, share):
+            engine, c0, c1 = share
+            nc.vector.quantize_mx(out=codes[:, c0:c1].bitcast(E4), scales=scales[:, c0:c1],
+                                  in_=st["il", key, c0][:].rearrange("p c j -> p (c j)"))
+
+        def dx_mm(b, j, n, passes):
+            cols = slice(512 * n, 512 * (n + 1))
+            for s in passes:
+                if s == 0:
+                    st["acc", b, j, n] = sum_bank()
+                nc.tensor.matmul_mx(out=st["acc", b, j, n][:], lhsT=st["zc", b, j][:, s, :].bitcast(E5),
+                                    lhsT_scale=st["zs", b, j][:, s, :], rhs=w_codes[s][:, cols].bitcast(E4),
+                                    rhs_scale=w_scales[s][:, cols], start=(s == 0), stop=(s == 2))
+
+        def leave(acc, rows, engines=("scalar", "scalar")):
+            res = work.tile([P, H], F32, name="res", tag="res", bufs=4)
+            for n in range(2):
+                dst = res[:, 512 * n:512 * (n + 1)]
+                if engines[n] == "scalar":
+                    nc.scalar.copy(out=dst, in_=acc[n][:])
+                else:
+                    nc.vector.tensor_copy(out=dst, in_=acc[n][:])
+            nc.sync.dma_start(out=rows, in_=res[:])
+
+        def dx_leave(b, j, engines=("scalar", "scalar")):
+            leave([st["acc", b, j, 0], st["acc", b, j, 1]], out_0[b].rearrange("(p j) h -> p j h", j=4)[:, j, :], engines)
+
+        def dw_tile(g, m, engines):
+            acc = [sum_bank(), sum_bank()]
+            rows = slice(P * m, P * (m + 1))
+            for n in range(2):
+                cols = slice(512 * n, 512 * (n + 1))
+                for b in range(B):
+                    nc.tensor.matmul_mx(out=acc[n][:], lhsT=d_codes[b][g][:, rows].bitcast(E5), lhsT_scale=d_scales[b][g][:, rows],
+                                        rhs=x_codes[b][:, cols].bitcast(E4), rhs_scale=x_scales[b][:, cols],
+                                        start=(b == 0), stop=(b == 1))
+            leave(acc, out_1[512 * g + P * m:512 * g + P * (m + 1), :], engines)
+
+        def il(op, engine, c0, c1):
+            interleave(op, (w_raw if op[0] == "w" else x_raw)[op[1]], (engine, c0, c1))
+
+        def qr(op, c0, c1):
+            codes, scales = (w_codes, w_scales) if op[0] == "w" else (x_codes, x_scales)
+            quant_rows(op, codes[op[1]], scales[op[1]], (None, c0, c1))
+
+        SV = ("scalar", "vector")
+        SS = ("scalar", "scalar")
+        def row_mm(b, j, passes=(0, 1, 3, 2)):
+            for n in range(2):
+                dx_mm(b, j, n, passes)
+
+        def row_turn(b, j):
+            turn_sum(b, j, 3)
+            turn_words(b, j, "scalar")
+
+        def row_products(b, j, following=None):
+            products_q(b, j, 1)
+            products(b, 3, j)
+            if following:
+                products_q(*following, 0)
+
+        W0, W1, W2, W3, X0, X1 = ("w", 0), ("w", 1), ("w", 2), ("w", 3), ("x", 0), ("x", 1)
+        G, SC, V = "gpsimd", "scalar", "vector"
+        VS = (V, SC)
+        negate(0)
+        table_turn(0)
+        table_back(0)
+        products(0, 0, 0, True)
+        products(0, 0, 1, True)
+        il(W0, G, 0, 384)
+        il(W0, SC, 384, 768)
+        turn_sum(0, 0, 0)
+        turn_sum(0, 1, 0)
+        products(0, 0, 2)
+        products(0, 0, 3)
+        il(W1, SC, 128, 640)
+        turn_sum(0, 2, 0)
+        il(W0, V, 768, 1024)
+        qr(W0, 0, 384)
+        qr(W0, 384, 768)
+        quant_z(0, 0, 0, 1)
+        quant_z(0, 1, 0, 1)
+        qr(W0, 768, 1024)
+        il(W1, V, 640, 1024)
+        load_x(0)
+        load_tables(1)
+        nc.sync.dma_start(out=g_a[1][:], in_=heads(grad_0, 1, 0))
+        turn_sum(0, 3, 0)
+        row_mm(0, 0, (0,))
+        row_mm(0, 1, (0,))
+        il(W1, G, 0, 128)
+        load_x(1)
+        nc.sync.dma_start(out=g_q[1][:], in_=heads(grad_0, 1, 4))
+        nc.sync.dma_start(out=g_k[1][:], in_=heads(grad_1, 1, 0))
+        nc.sync.dma_start(out=g_v[1][:], in_=heads(grad_2, 1, 0))
+        products_q(0, 0, 0)
+        row_products(0, 0, (0, 1))
+        il(W3, SC, 128, 640)
+        qr(W1, 640, 1024)
+        qr(W1, 128, 640)
+        sort_v(0)
+        qr(W1, 0, 128)
+        il(W3, SC, 640, 1024)
+        row_turn(0, 0)
+        il(W3, G, 0, 128)
+        row_products(0, 1, (0, 2))
+        il(W2, SC, 128, 640)
+        il(W2, V, 640, 1024)
+        qr(W3, 128, 640)
+        qr(W3, 640, 1024)
+        qr(W2, 640, 1024)
+        quant_z(0, 0, 1, 3)
+        quant_z(0, 0, 3, 4)
+        qr(W3, 0, 128)
+        row_turn(0, 1)
+        row_mm(0, 0, (1, 3))
+        il(W2, G, 0, 128)
+        row_products(0, 2, (0, 3))
+        qr(W2, 128, 640)
+        negate(1)
+        quant_z(0, 1, 1, 3)
+        quant_z(0, 1, 3, 4)
+        qr(W2, 0, 128)
+        row_turn(0, 2)
+        row_mm(0, 0, (2,))
+        table_turn(1)
+        row_mm(0, 1, (1, 3, 2))
+        dx_leave(0, 0)
+        il(X0, G, 0, 128)
+        row_products(0, 3)
+        dx_leave(0, 1, VS)
+        quant_z(0, 2, 0, 4)
+        qr(X0, 0, 128)
+        table_back(1)
+        row_turn(0, 3)
+        turn_back(0, 0, SC)
+        row_mm(0, 2)
+        dx_leave(0, 2)
+        il(X0, G, 128, 384)
+        products(1, 0, 0)
+        products_q(1, 0, 0)
+        row_products(1, 0)
+        sort_v(1)
+        quant_z(0, 3, 0, 4)
+        qr(X0, 128, 384)
+        turn_sum(1, 0, 0)
+        row_turn(1, 0)
+        il(X0, SC, 384, 640)
+        row_mm(0, 3)
+        turn_back(0, 1, SC)
+        dx_leave(0, 3)
+        il(X1, G, 0, 512)
+        products(1, 0, 1)
+        products(1, 0, 2)
+        products(1, 0, 3)
+        products_q(1, 1, 0)
+        il(X0, V, 640, 1024)
+        quant_z(1, 0, 0, 4)
+        qr(X0, 384, 640)
+        quant_d(0, 0)
+        qr(X0, 640, 1024)
+        qr(X1, 0, 512)
+        turn_sum(1, 1, 0)
+        turn_sum(1, 2, 0)
+        turn_sum(1, 3, 0)
+        il(X1, SC, 640, 1024)
+        row_mm(1, 0)
+        turn_back(1, 0, SC)
+        turn_back(1, 1, SC)
+        dx_leave(1, 0)
+        il(X1, G, 512, 640)
+        row_products(1, 1, (1, 2))
+        qr(X1, 640, 1024)
+        qr(X1, 512, 640)
+        quant_d(1, 0)
+        row_turn(1, 1)
+        d_interleave(0, SC, 0, 256)
+        dw_tile(0, 0, SS)
+        dw_tile(0, 1, SS)
+        row_products(1, 2, (1, 3))
+        quant_z(1, 1, 0, 4)
+        row_turn(1, 2)
+        d_interleave(0, SC, 256, 512)
+        row_mm(1, 1)
+        dx_leave(1, 1)
+        dw_tile(0, 2, SS)
+        row_products(1, 3)
+        quant_z(1, 2, 0, 4)
+        d_interleave(1, V, 0, 512)
+        quant_d(0, 1)
+        row_turn(1, 3)
+        quant_d(1, 1)
+        quant_z(1, 3, 0, 4)
+        row_mm(1, 2)
+        dx_leave(1, 2, SV)
+        dw_tile(0, 3, SV)
+        row_mm(1, 3)
+        dx_leave(1, 3, SV)
+        for m in range(4):
+            dw_tile(1, m, SV)

@@ -28,12 +28,12 @@ def tile_mistralattention_v_kernel(tc, hidden_states, cos, sin, q_w, k_w, v_w, g
         def kept(shape, dtype, name):
             return keep.tile(shape, dtype, name=name, align_bytes=64)
 
-        tab = [kept([P, 2, 512], BF16, "tab%d" % b) for b in range(B)]
-        sin_raw = [kept([P, 4, 2, 64], BF16, "sin%d" % b) for b in range(B)]
-        g_a = [kept([P, 4, 512], BF16, "ga%d" % b) for b in range(B)]
-        g_q = [kept([P, 4, 512], BF16, "gq%d" % b) for b in range(B)]
-        g_k = [kept([P, 4, 512], BF16, "gk%d" % b) for b in range(B)]
-        g_v = [kept([P, 4, 512], BF16, "gv%d" % b) for b in range(B)]
+        tab = kept([P, B * 1024], BF16, "tab")[:].rearrange("p (b s c) -> p b s c", b=B, s=2)
+        sin_raw = kept([P, B * 4, 2, 64], BF16, "sin")
+        g_a = work.tile([P, 4, 512], BF16, name="ga", tag="g4", bufs=2)
+        g_k = [work.tile([P, 4, 512], BF16, name="gk0", tag="g4", bufs=2)]
+        g_q = [kept([P, 4, 512], BF16, "gq0"), kept([P, 4096], BF16, "gq1")[:].rearrange("p (h c) -> p h c", h=8)]
+        g_v = {}
         w_raw = [work.tile([P, 4, H], BF16, name="wraw%d" % s, tag="raw", bufs=4) for s in range(4)]
         x_raw = []
         w_codes = [kept([P, H], U32, "wc%d" % s) for s in range(4)]
@@ -47,9 +47,22 @@ def tile_mistralattention_v_kernel(tc, hidden_states, cos, sin, q_w, k_w, v_w, g
         def heads(grad, b, h0):
             return grad[b, h0:h0 + 4].rearrange("h (p j) d -> p h (j d)", j=4)
 
-        def load_tables(b):
-            nc.sync.dma_start(out=tab[b][:, 0, :], in_=cos[b].rearrange("(p j) d -> p (j d)", j=4))
-            nc.sync.dma_start(out=sin_raw[b][:].rearrange("p j a i -> p (j a i)"), in_=sin[b].rearrange("(p j) d -> p (j d)", j=4))
+        def load_v(b, j):
+            g_v[b, j] = work.tile([P, 512], BF16, name="gv", tag="gv", bufs=6)
+            nc.sync.dma_start(out=g_v[b, j][:].rearrange("p (h d) -> p h d", h=4),
+                              in_=grad_2[b].rearrange("h (p j) d -> p j h d", j=4)[:, j])
+
+        def load_k1():
+            g_k.append(work.tile([P, 4, 512], BF16, name="gk1", tag="g4", bufs=2))
+            nc.sync.dma_start(out=g_k[1][:], in_=heads(grad_1, 1, 0))
+
+        def load_q1():
+            nc.sync.dma_start(out=g_q[1][:, 0:4, :], in_=heads(grad_0, 1, 0))
+            nc.sync.dma_start(out=g_q[1][:, 4:8, :], in_=heads(grad_0, 1, 4))
+
+        def load_tables():
+            nc.sync.dma_start(out=tab[:, :, 0, :], in_=cos.rearrange("b (p j) d -> p b (j d)", j=4))
+            nc.sync.dma_start(out=sin_raw[:].rearrange("p (b j) a i -> p b (j a i)", b=B), in_=sin.rearrange("b (p j) d -> p b (j d)", j=4))
 
         w_rows = [q_w[0:512, :], q_w[512:1024, :], v_w, k_w]
 
@@ -60,48 +73,55 @@ def tile_mistralattention_v_kernel(tc, hidden_states, cos, sin, q_w, k_w, v_w, g
             x_raw.append(work.tile([P, 4, H], BF16, name="xraw%d" % b, tag="raw", bufs=4))
             nc.sync.dma_start(out=x_raw[b][:], in_=hidden_states[b].rearrange("(p j) h -> p j h", j=4))
 
-        load_tables(0)
-        nc.sync.dma_start(out=g_a[0][:], in_=heads(grad_0, 0, 0))
+        load_tables()
         load_w(0)
+        nc.sync.dma_start(out=g_a[:], in_=heads(grad_0, 0, 0))
         load_w(1)
+        load_w(3)
         nc.sync.dma_start(out=g_q[0][:], in_=heads(grad_0, 0, 4))
         nc.sync.dma_start(out=g_k[0][:], in_=heads(grad_1, 0, 0))
-        load_w(3)
-        nc.sync.dma_start(out=g_v[0][:], in_=heads(grad_2, 0, 0))
+        load_v(0, 0)
         load_w(2)
+        load_v(0, 1)
+        load_v(0, 2)
+        load_v(0, 3)
         make_identity(nc, ident[:])
 
         def turn_bank():
-            return psum.tile([P, 4, P], F32, name="turn", tag="turn", bufs=3)
+            st["turns"] = st.get("turns", 0) + 1
+            return psum.tile([P, 4, P], F32, name="turn", tag="turn%d" % (st["turns"] % 3), bufs=1)
 
         def sum_bank():
-            return psum.tile([P, 512], F32, name="sums", tag="sums", bufs=4)
+            tags = st["sum_tags"]
+            st["sums"] = st.get("sums", 0) + 1
+            return psum.tile([P, 512], F32, name="sums", tag=tags[st["sums"] % len(tags)], bufs=1)
 
         st = {}
 
-        def negate(b):
-            dst = tab[b][:, 1, :].rearrange("p (j a i) -> p j a i", j=4, a=2)
-            nc.vector.tensor_copy(out=dst[:, :, 0, :], in_=sin_raw[b][:, :, 1, :])
-            nc.vector.tensor_scalar(out=dst[:, :, 1, :], in0=sin_raw[b][:, :, 0, :], scalar1=-1.0, scalar2=None, op0=MULT)
+        def negate():
+            dst = tab[:, :, 1, :].rearrange("p b (j a i) -> p b j a i", j=4, a=2)
+            src = sin_raw[:].rearrange("p (b j) a i -> p b j a i", b=B)
+            nc.vector.tensor_copy(out=dst[:, :, :, 0, :], in_=src[:, :, :, 1, :])
+            nc.vector.tensor_scalar(out=dst[:, :, :, 1, :], in0=src[:, :, :, 0, :], scalar1=-1.0, scalar2=None, op0=MULT)
 
         def table_turn(b):
             bank = turn_bank()
-            words = tab[b][:].rearrange("p s c -> p (s c)").bitcast(F32)
+            words = tab[:, b].rearrange("p s c -> p (s c)").bitcast(F32)
             for c in range(4):
                 nc.tensor.transpose(bank[:, c, :], words[:, c * P:(c + 1) * P], ident[:])
-            turned = work.tile([P, 4, P], F32, name="tabT", tag="tabT", bufs=1)
+            turned = work.tile([P, 4, P], F32, name="tabT", tag="t1", bufs=3)
             nc.scalar.copy(out=turned[:], in_=bank[:])
             st["tabT", b] = turned
 
         def table_back(b):
-            bank = psum.tile([P, 4, P], F32, name="table", tag="table", bufs=1)
+            bank = psum.tile([P, 4, P], F32, name="table", tag="table%d" % b, bufs=1)
             for c in range(4):
                 nc.tensor.transpose(bank[:, c, :], st["tabT", b][:, c, :], ident[:])
             st["table", b] = bank[:].rearrange("p c w -> p (c w)").bitcast(BF16)
 
         def products(b, s, j, from_sbuf=False):
-            g = g_a[b][:] if s == 0 else g_k[b][:]
-            table = tab[b][:].rearrange("p s c -> p (s c)") if from_sbuf else st["table", b]
+            g = g_a[:] if s == 0 else g_k[b][:]
+            table = tab[:, b].rearrange("p s c -> p (s c)") if from_sbuf else st["table", b]
             table = table.rearrange("p (s j m t) -> p s j t m", s=2, j=4, t=4)
             gv = g.rearrange("p h (j m t) -> p j t h m", j=4, t=4)[:, j]
             t1 = work.tile([P, 4, 4, 32], F32, name="t1", tag="t1", bufs=3)
@@ -115,46 +135,46 @@ def tile_mistralattention_v_kernel(tc, hidden_states, cos, sin, q_w, k_w, v_w, g
             st["t", b, s, j] = (t1, t2)
 
         def products_q(b, j, part):
+            nh = g_q[b].shape[1]
             table = st["table", b].rearrange("p (s j a i) -> p s j a i", s=2, j=4, a=2)
             gv = g_q[b][:].rearrange("p h (j a i) -> p j h a i", j=4, a=2)[:, j]
-            u = work.tile([P, 4, 2, 64], F32, name="u%d" % part, tag="u%d" % part, bufs=2)
+            u = work.tile([P, nh, 2, 64], F32, name="u%d" % part, tag="u%d" % part, bufs=2)
             nc.vector.tensor_tensor(out=u[:], in0=gv[:, :, ::-1, :] if part else gv,
-                                    in1=table[:, part, j].unsqueeze(1).to_broadcast([P, 4, 2, 64]), op=MULT)
-            st["u", part] = u
-            if part == 1:
-                if j == 0:
-                    st["dq", b] = work.tile([P, 4, 512], BF16, name="dq", tag="dq", bufs=2)
-                nc.gpsimd.tensor_tensor(out=st["dq", b][:, j, :], in0=st["u", 0][:].rearrange("p h a i -> p (h a i)"),
-                                        in1=u[:].rearrange("p h a i -> p (h a i)"), op=ADD)
+                                    in1=table[:, part, j].unsqueeze(1).to_broadcast([P, nh, 2, 64]), op=MULT)
+            st["u", b, j, part] = u
 
-        def turn_words(b, j, engine):
+        def add_q(b, j):
+            if j == 0:
+                st["dq", b] = kept([P, 4 * P * g_q[b].shape[1]], BF16, "dq%d" % b)[:].rearrange("p (j c) -> p j c", j=4)
+            nc.gpsimd.tensor_tensor(out=st["dq", b][:, j, :], in0=st["u", b, j, 0][:].rearrange("p h a i -> p (h a i)"),
+                                    in1=st["u", b, j, 1][:].rearrange("p h a i -> p (h a i)"), op=ADD)
+
+        def turn_words(b, j, s0, s1, engine):
             bank = turn_bank()
-            for u in range(2):
-                nc.tensor.transpose(bank[:, 2 + u, :], st["vs", b][:, j, u, :], ident[:])
-            for u in range(2):
-                nc.tensor.transpose(bank[:, u, :], st["dq", b][:, j, :].bitcast(F32)[:, u:256:2], ident[:])
+            for s in range(s0, s1):
+                src = g_v[b, j][:] if s == 2 else st["dq", b][:, j, 512 * (s - 1 + b):512 * (s + b)]
+                for u in range(2):
+                    nc.tensor.transpose(bank[:, 2 * (s - s0) + u, :], src.bitcast(F32)[:, u:256:2], ident[:])
             z = z_tile(b, j)
-            dst = z[:, 1:3, :].bitcast(F32).rearrange("p s (c u) -> p s c u", u=2)
-            src = bank[:].rearrange("p (s u) c -> p s c u", u=2)
+            dst = z[:, s0:s1, :].bitcast(F32).rearrange("p s (c u) -> p s c u", u=2)
+            src = bank[:, 0:2 * (s1 - s0), :].rearrange("p (s u) c -> p s c u", u=2)
             if engine == "scalar":
                 nc.scalar.copy(out=dst, in_=src)
             else:
                 nc.vector.tensor_copy(out=dst, in_=src)
 
-        def d_interleave(b, engine, c0, c1):
+        def d_interleave(b, g, engine, c0, c1):
             if c0 == 0:
-                st["d", b, 1] = work.tile([P, 512, 4], BF16, name="d", tag="d", bufs=2, align_bytes=64)
-            src = st["dq", b][:, :, c0:c1].rearrange("p j c -> p c j")
-            if engine == "scalar":
-                nc.scalar.copy(out=st["d", b, 1][:, c0:c1, :], in_=src)
-            else:
-                nc.vector.tensor_copy(out=st["d", b, 1][:, c0:c1, :], in_=src)
+                st["d", b, g] = work.tile([P, 512, 4], BF16, name="d", tag="d", bufs=3, align_bytes=64)
+            off = 512 * (g - 1 + b)
+            weave(engine, st["d", b, g][:, c0:c1, :], st["dq", b][:, :, off + c0:off + c1])
 
         def z_tile(b, j):
             if ("z", b, j) not in st:
-                st["z", b, j] = work.tile([P, 4, 512], BF16, name="z%d%d" % (b, j), tag="z", bufs=8, align_bytes=64)
-                st["zc", b, j] = work.tile([P, 4, P], U32, name="zc", tag="zc", bufs=6, align_bytes=64)
-                st["zs", b, j] = work.tile([P, 4, P], U8, name="zs", tag="zs", bufs=6, align_bytes=64)
+                z = work.tile([P, 2048], BF16, name="z%d%d" % (b, j), tag="z", bufs=6, align_bytes=64)
+                st["z", b, j] = z[:].rearrange("p (s c) -> p s c", s=4)
+                st["zc", b, j] = work.tile([P, 4, P], U32, name="zc", tag="zc", bufs=4, align_bytes=64)
+                st["zs", b, j] = work.tile([P, 4, P], U8, name="zs", tag="zs", bufs=4, align_bytes=64)
             return st["z", b, j]
 
         def turn_sum(b, j, s):
@@ -167,13 +187,6 @@ def tile_mistralattention_v_kernel(tc, hidden_states, cos, sin, q_w, k_w, v_w, g
             z = z_tile(b, j)
             nc.scalar.copy(out=z[:, s, :].rearrange("p (c t) -> p c t", t=4), in_=bank[:].rearrange("p t c -> p c t"))
 
-        def sort_v(b):
-            vs = work.tile([P, 4, 2, P], F32, name="vs", tag="vs", bufs=1)
-            words = g_v[b][:].bitcast(F32).rearrange("p h (j m u) -> p j u h m", j=4, u=2)
-            for u in range(2):
-                nc.vector.tensor_copy(out=vs[:, :, u, :].rearrange("p j (h m) -> p j h m", h=4), in_=words[:, :, u])
-            st["vs", b] = vs
-
         def quant_z(b, j, s0, s1):
             nc.vector.quantize_mx(out=st["zc", b, j][:, s0:s1, :].rearrange("p s c -> p (s c)").bitcast(E5),
                                   scales=st["zs", b, j][:, s0:s1, :].rearrange("p s c -> p (s c)"),
@@ -181,7 +194,7 @@ def tile_mistralattention_v_kernel(tc, hidden_states, cos, sin, q_w, k_w, v_w, g
 
         def turn_back(b, u, engine):
             if u == 0:
-                st["d", b, 0] = work.tile([P, 512, 4], BF16, name="d", tag="d", bufs=2, align_bytes=64)
+                st["d", b, 0] = work.tile([P, 512, 4], BF16, name="d", tag="d", bufs=3, align_bytes=64)
             bank = turn_bank()
             for j in range(4):
                 nc.tensor.transpose(bank[:, j, :], st["z", b, j][:, 0, :].bitcast(F32)[:, u:256:2], ident[:])
@@ -192,21 +205,27 @@ def tile_mistralattention_v_kernel(tc, hidden_states, cos, sin, q_w, k_w, v_w, g
             else:
                 nc.vector.tensor_copy(out=dst, in_=src)
 
-        def quant_d(b, g):
-            nc.vector.quantize_mx(out=d_codes[b][g][:].bitcast(E5), scales=d_scales[b][g][:],
-                                  in_=st["d", b, g][:].rearrange("p c j -> p (c j)"))
+        def quant_d(b, g, c0=0, c1=512):
+            nc.vector.quantize_mx(out=d_codes[b][g][:, c0:c1].bitcast(E5), scales=d_scales[b][g][:, c0:c1],
+                                  in_=st["d", b, g][:, c0:c1, :].rearrange("p c j -> p (c j)"))
 
-        def interleave(key, raw, share):
+        def weave(engine, dst, src):
+            dst = dst.rearrange("p (c i) j -> p c j i", i=4)
+            src = src.rearrange("p j (c i) -> p c j i", i=4)
+            if engine == "scalar":
+                nc.scalar.copy(out=dst, in_=src)
+            else:
+                nc.vector.tensor_copy(out=dst, in_=src)
+
+        def interleave(key, raw, share, slot):
             engine, c0, c1 = share
-            stage = work.tile([P, c1 - c0, 4], BF16, name="il" + engine, tag="il" + engine,
-                              bufs={"gpsimd": 1, "scalar": 3, "vector": 1}[engine], align_bytes=64)
+            stage = work.tile([P, c1 - c0, 4], BF16, name="il" + slot, tag="il" + slot,
+                              bufs={"gpsimd": 1, "head": 1, "late": 3, "scalar": 5, "vector": 1}[slot], align_bytes=64)
             src = raw[:, :, c0:c1].rearrange("p j c -> p c j")
             if engine == "gpsimd":
                 nc.gpsimd.tensor_scalar(out=stage[:], in0=src, scalar1=1.0, scalar2=0.0, op0=MULT, op1=ADD)
-            elif engine == "scalar":
-                nc.scalar.copy(out=stage[:], in_=src)
             else:
-                nc.vector.tensor_copy(out=stage[:], in_=src)
+                weave(engine, stage[:], raw[:, :, c0:c1])
             st["il", key, c0] = stage
 
         def quant_rows(key, codes, scales, share):
@@ -223,15 +242,18 @@ def tile_mistralattention_v_kernel(tc, hidden_states, cos, sin, q_w, k_w, v_w, g
                                     lhsT_scale=st["zs", b, j][:, s, :], rhs=w_codes[s][:, cols].bitcast(E4),
                                     rhs_scale=w_scales[s][:, cols], start=(s == 0), stop=(s == 2))
 
-        def leave(acc, rows, engines=("scalar", "scalar")):
-            res = work.tile([P, H], F32, name="res", tag="res", bufs=4)
+        def leave(acc, rows, engines=("scalar", "scalar"), halves=False, tag="res"):
+            res = work.tile([P, H], F32, name="res", tag=tag, bufs=4)
             for n in range(2):
-                dst = res[:, 512 * n:512 * (n + 1)]
+                cols = slice(512 * n, 512 * (n + 1))
                 if engines[n] == "scalar":
-                    nc.scalar.copy(out=dst, in_=acc[n][:])
+                    nc.scalar.copy(out=res[:, cols], in_=acc[n][:])
                 else:
-                    nc.vector.tensor_copy(out=dst, in_=acc[n][:])
-            nc.sync.dma_start(out=rows, in_=res[:])
+                    nc.vector.tensor_copy(out=res[:, cols], in_=acc[n][:])
+                if halves:
+                    nc.sync.dma_start(out=rows[:, cols], in_=res[:, cols])
+            if not halves:
+                nc.sync.dma_start(out=rows, in_=res[:])
 
         def dx_leave(b, j, engines=("scalar", "scalar")):
             leave([st["acc", b, j, 0], st["acc", b, j, 1]], out_0[b].rearrange("(p j) h -> p j h", j=4)[:, j, :], engines)
@@ -245,10 +267,10 @@ def tile_mistralattention_v_kernel(tc, hidden_states, cos, sin, q_w, k_w, v_w, g
                     nc.tensor.matmul_mx(out=acc[n][:], lhsT=d_codes[b][g][:, rows].bitcast(E5), lhsT_scale=d_scales[b][g][:, rows],
                                         rhs=x_codes[b][:, cols].bitcast(E4), rhs_scale=x_scales[b][:, cols],
                                         start=(b == 0), stop=(b == 1))
-            leave(acc, out_1[512 * g + P * m:512 * g + P * (m + 1), :], engines)
+            leave(acc, out_1[512 * g + P * m:512 * g + P * (m + 1), :], engines, g == 1 and m == 3, "raw" if g == 0 else "res")
 
-        def il(op, engine, c0, c1):
-            interleave(op, (w_raw if op[0] == "w" else x_raw)[op[1]], (engine, c0, c1))
+        def il(op, engine, c0, c1, slot=None):
+            interleave(op, (w_raw if op[0] == "w" else x_raw)[op[1]], (engine, c0, c1), slot or engine)
 
         def qr(op, c0, c1):
             codes, scales = (w_codes, w_scales) if op[0] == "w" else (x_codes, x_scales)
@@ -256,156 +278,137 @@ def tile_mistralattention_v_kernel(tc, hidden_states, cos, sin, q_w, k_w, v_w, g
 
         SV = ("scalar", "vector")
         SS = ("scalar", "scalar")
-        def row_mm(b, j, passes=(0, 1, 3, 2)):
-            for n in range(2):
-                dx_mm(b, j, n, passes)
-
-        def row_turn(b, j):
-            turn_sum(b, j, 3)
-            turn_words(b, j, "scalar")
-
-        def row_products(b, j, following=None):
-            products_q(b, j, 1)
-            products(b, 3, j)
-            if following:
-                products_q(*following, 0)
-
         W0, W1, W2, W3, X0, X1 = ("w", 0), ("w", 1), ("w", 2), ("w", 3), ("x", 0), ("x", 1)
         G, SC, V = "gpsimd", "scalar", "vector"
         VS = (V, SC)
-        negate(0)
+        ALL = (0, 1, 3, 2)
+        def row_products(b, j):
+            products_q(b, j, 0)
+            products_q(b, j, 1)
+
+        def row_mm(r):
+            dx_mm(r // 4, r % 4, 0, ALL)
+            dx_mm(r // 4, r % 4, 1, ALL)
+
+        def row_turn(r, engine=SC):
+            turn_sum(r // 4, r % 4, 3)
+            if r < 4:
+                turn_words(0, r, 1, 3, engine)
+            else:
+                turn_words(1, r % 4, 2, 3, engine)
+                turn_words(1, r % 4, 0, 2, engine)
+
+        def row_leave(r, engines=SS):
+            dx_leave(r // 4, r % 4, engines)
+
+        def row_quant(r):
+            quant_z(r // 4, r % 4, 0, 4)
+
+        THIRDS = ((0, 384), (384, 768), (768, 1024))
+        st["sum_tags"] = ["sum0", "sum1", "sum2", "table0"]
+        negate()
         table_turn(0)
-        table_back(0)
-        products(0, 0, 0, True)
-        products(0, 0, 1, True)
-        il(W0, G, 0, 384)
-        il(W0, SC, 384, 768)
-        turn_sum(0, 0, 0)
-        turn_sum(0, 1, 0)
-        products(0, 0, 2)
-        products(0, 0, 3)
-        il(W1, SC, 128, 640)
-        turn_sum(0, 2, 0)
-        il(W0, V, 768, 1024)
-        qr(W0, 0, 384)
-        qr(W0, 384, 768)
-        quant_z(0, 0, 0, 1)
-        quant_z(0, 1, 0, 1)
-        qr(W0, 768, 1024)
-        il(W1, V, 640, 1024)
-        load_x(0)
-        load_tables(1)
-        nc.sync.dma_start(out=g_a[1][:], in_=heads(grad_0, 1, 0))
-        turn_sum(0, 3, 0)
-        row_mm(0, 0, (0,))
-        row_mm(0, 1, (0,))
-        il(W1, G, 0, 128)
-        load_x(1)
-        nc.sync.dma_start(out=g_q[1][:], in_=heads(grad_0, 1, 4))
-        nc.sync.dma_start(out=g_k[1][:], in_=heads(grad_1, 1, 0))
-        nc.sync.dma_start(out=g_v[1][:], in_=heads(grad_2, 1, 0))
-        products_q(0, 0, 0)
-        row_products(0, 0, (0, 1))
-        il(W3, SC, 128, 640)
-        qr(W1, 640, 1024)
-        qr(W1, 128, 640)
-        sort_v(0)
-        qr(W1, 0, 128)
-        il(W3, SC, 640, 1024)
-        row_turn(0, 0)
-        il(W3, G, 0, 128)
-        row_products(0, 1, (0, 2))
-        il(W2, SC, 128, 640)
-        il(W2, V, 640, 1024)
-        qr(W3, 128, 640)
-        qr(W3, 640, 1024)
-        qr(W2, 640, 1024)
-        quant_z(0, 0, 1, 3)
-        quant_z(0, 0, 3, 4)
-        qr(W3, 0, 128)
-        row_turn(0, 1)
-        row_mm(0, 0, (1, 3))
-        il(W2, G, 0, 128)
-        row_products(0, 2, (0, 3))
-        qr(W2, 128, 640)
-        negate(1)
-        quant_z(0, 1, 1, 3)
-        quant_z(0, 1, 3, 4)
-        qr(W2, 0, 128)
-        row_turn(0, 2)
-        row_mm(0, 0, (2,))
         table_turn(1)
-        row_mm(0, 1, (1, 3, 2))
-        dx_leave(0, 0)
-        il(X0, G, 0, 128)
-        row_products(0, 3)
-        dx_leave(0, 1, VS)
-        quant_z(0, 2, 0, 4)
-        qr(X0, 0, 128)
+        table_back(0)
         table_back(1)
-        row_turn(0, 3)
+        il(W0, V, 768, 1024, "head")
+        il(W0, SC, 384, 768)
+        qr(W0, 768, 1024)
+        il(W0, G, 0, 384, "head")
+        il(W1, G, 0, 384)
+        il(W1, SC, 384, 768)
+        load_q1()
+        products(0, 0, 0)
+        turn_sum(0, 0, 0)
+        products(0, 0, 1)
+        turn_sum(0, 1, 0)
+        il(W1, SC, 768, 1024)
+        products(0, 0, 2)
+        turn_sum(0, 2, 0)
+        products(0, 0, 3)
+        load_k1()
+        load_v(1, 0)
+        load_v(1, 1)
+        load_x(0)
+        load_x(1)
+        qr(W0, 384, 768)
+        qr(W1, 384, 768)
+        qr(W1, 0, 384)
+        qr(W0, 0, 384)
+        turn_sum(0, 3, 0)
+        il(W3, G, 0, 384, "head")
+        il(W3, SC, 384, 768)
         turn_back(0, 0, SC)
-        row_mm(0, 2)
-        dx_leave(0, 2)
-        il(X0, G, 128, 384)
-        products(1, 0, 0)
-        products_q(1, 0, 0)
-        row_products(1, 0)
-        sort_v(1)
-        quant_z(0, 3, 0, 4)
-        qr(X0, 128, 384)
-        turn_sum(1, 0, 0)
-        row_turn(1, 0)
-        il(X0, SC, 384, 640)
-        row_mm(0, 3)
+        il(W3, SC, 768, 1024)
+        products_q(0, 0, 0)
+        for j in range(4):
+            products_q(0, j, 1)
+            add_q(0, j)
+            products(0, 3, j)
+            products_q((j + 1) // 4, (j + 1) % 4, 0)
+            if j == 1:
+                il(W2, G, 0, 384)
+            if j < 3:
+                row_turn(j)
+            if j == 0:
+                il(W2, SC, 384, 768)
+            if j == 1:
+                load_v(1, 2)
+                load_v(1, 3)
+                il(W2, SC, 768, 1024)
+        row_quant(0)
+        qr(W1, 768, 1024)
+        for op in (W3, W2):
+            for c0, c1 in THIRDS:
+                qr(op, c0, c1)
+        row_quant(1)
         turn_back(0, 1, SC)
-        dx_leave(0, 3)
-        il(X1, G, 0, 512)
-        products(1, 0, 1)
-        products(1, 0, 2)
-        products(1, 0, 3)
-        products_q(1, 1, 0)
-        il(X0, V, 640, 1024)
-        quant_z(1, 0, 0, 4)
-        qr(X0, 384, 640)
-        quant_d(0, 0)
-        qr(X0, 640, 1024)
-        qr(X1, 0, 512)
-        turn_sum(1, 1, 0)
-        turn_sum(1, 2, 0)
-        turn_sum(1, 3, 0)
-        il(X1, SC, 640, 1024)
-        row_mm(1, 0)
-        turn_back(1, 0, SC)
-        turn_back(1, 1, SC)
-        dx_leave(1, 0)
-        il(X1, G, 512, 640)
-        row_products(1, 1, (1, 2))
+        d_interleave(0, 1, SC, 0, 256)
+        row_mm(0)
+        row_leave(0)
+        row_turn(3)
+        XS = ((X0, 0, 256), (X0, 256, 512), (X0, 512, 768), (X1, 0, 256), (X1, 256, 512))
+        XG = ((X0, 768, 896), (X0, 896, 1024), (X1, 512, 640))
+        il(XS[0][0], SC, XS[0][1], XS[0][2])
+        row_mm(1)
+        row_leave(1)
+        for j in range(4):
+            r = 4 + j
+            products_q(1, j, 1)
+            row_quant(r - 2)
+            add_q(1, j)
+            products(1, 3, j)
+            if j < 3:
+                il(XG[j][0], G, XG[j][1], XG[j][2], "late")
+                products_q(1, j + 1, 0)
+            row_turn(r)
+            if j < 3:
+                il(XS[1 + j][0], SC, XS[1 + j][1], XS[1 + j][2])
+            row_mm(r - 2)
+            if j == 1:
+                d_interleave(0, 1, SC, 256, 512)
+            row_leave(r - 2)
+        il(XS[4][0], V, XS[4][1], XS[4][2], SC)
+        il(X1, V, 640, 1024)
+        row_quant(6)
+        d_interleave(1, 0, V, 0, 512)
+        for op, c0, c1 in XG + XS[:3]:
+            qr(op, c0, c1)
+        row_quant(7)
+        for op, c0, c1 in XS[3:]:
+            qr(op, c0, c1)
         qr(X1, 640, 1024)
-        qr(X1, 512, 640)
         quant_d(1, 0)
-        row_turn(1, 1)
-        d_interleave(0, SC, 0, 256)
-        dw_tile(0, 0, SS)
-        dw_tile(0, 1, SS)
-        row_products(1, 2, (1, 3))
-        quant_z(1, 1, 0, 4)
-        row_turn(1, 2)
-        d_interleave(0, SC, 256, 512)
-        row_mm(1, 1)
-        dx_leave(1, 1)
-        dw_tile(0, 2, SS)
-        row_products(1, 3)
-        quant_z(1, 2, 0, 4)
-        d_interleave(1, V, 0, 512)
+        quant_d(0, 0)
+        row_mm(6)
+        row_leave(6)
         quant_d(0, 1)
-        row_turn(1, 3)
+        d_interleave(1, 1, V, 0, 512)
+        row_mm(7)
+        st["sum_tags"] = ["turn0", "turn1", "turn2", "table1", "sum0", "sum1", "sum2", "table0"]
+        st["sums"] = -1
+        row_leave(7)
         quant_d(1, 1)
-        quant_z(1, 3, 0, 4)
-        row_mm(1, 2)
-        dx_leave(1, 2, SV)
-        dw_tile(0, 3, SV)
-        row_mm(1, 3)
-        dx_leave(1, 3, SV)
-        for m in range(4):
-            dw_tile(1, m, SV)
+        for g in range(2):
+            for m in range(4):
+                dw_tile(g, m, SV)

@@ -3,412 +3,377 @@ from contextlib import ExitStack
 import concourse.mybir as mybir
 from concourse.masks import make_identity
 
-B, S, H, HD = 2, 512, 1024, 128
+B, H = 2, 1024
 FLOPS = 2 * 1024 * 2048 * 1024 + 2 * 1024 * 1024 * 1024
 
 F32 = mybir.dt.float32
 BF16 = mybir.dt.bfloat16
 U32 = mybir.dt.uint32
 U8 = mybir.dt.uint8
-E4 = mybir.dt.float8_e4m3fn_x4
-E5 = mybir.dt.float8_e5m2_x4
+E4M3 = mybir.dt.float8_e4m3fn_x4
+E5M2 = mybir.dt.float8_e5m2_x4
 MULT = mybir.AluOpType.mult
 ADD = mybir.AluOpType.add
+
 P = 128
+PASS = 512
+Q_LO, Q_HI, V_PASS, K_PASS = 0, 1, 2, 3
+PASS_ORDER = (Q_LO, Q_HI, K_PASS, V_PASS)
+SCALAR, VECTOR, GPSIMD = "scalar", "vector", "gpsimd"
+
+W_GPSIMD = 384
+W_CUT = 768
+W_FIRST_GPSIMD = 640
+X_SCALAR = 256
+X_GPSIMD = 128
 
 
-def tile_mistralattention_v_kernel(tc, hidden_states, cos, sin, q_w, k_w, v_w, grad_0, grad_1, grad_2, out_0, out_1):
+def tile_mistralattention_v_kernel(tc, hidden_states, cos, sin, q_w, k_w, v_w, grad_0, grad_1, grad_2,
+                                                out_0, out_1):
     nc = tc.nc
     with ExitStack() as ctx:
         keep = ctx.enter_context(tc.tile_pool(name="keep", bufs=1))
-        work = ctx.enter_context(tc.tile_pool(name="work", bufs=2))
+        work = ctx.enter_context(tc.tile_pool(name="work", bufs=1))
         psum = ctx.enter_context(tc.psum_pool(name="psum", bufs=1))
         ctx.enter_context(tc.manual_schedule())
 
         def kept(shape, dtype, name):
             return keep.tile(shape, dtype, name=name, align_bytes=64)
 
-        tab = kept([P, B * 1024], BF16, "tab")[:].rearrange("p (b s c) -> p b s c", b=B, s=2)
-        sin_raw = kept([P, B * 4, 2, 64], BF16, "sin")
-        g_a = work.tile([P, 4, 512], BF16, name="ga", tag="g4", bufs=2)
-        g_k = [work.tile([P, 4, 512], BF16, name="gk0", tag="g4", bufs=2)]
-        g_q = [kept([P, 4, 512], BF16, "gq0"), kept([P, 4096], BF16, "gq1")[:].rearrange("p (h c) -> p h c", h=8)]
-        g_v = {}
-        w_raw = [work.tile([P, 4, H], BF16, name="wraw%d" % s, tag="raw", bufs=4) for s in range(4)]
-        x_raw = []
-        w_codes = [kept([P, H], U32, "wc%d" % s) for s in range(4)]
-        w_scales = [kept([P, H], U8, "ws%d" % s) for s in range(4)]
-        x_codes = [kept([P, H], U32, "xc%d" % b) for b in range(B)]
-        x_scales = [kept([P, H], U8, "xs%d" % b) for b in range(B)]
-        d_codes = [[kept([P, 512], U32, "dc%d%d" % (b, g)) for g in range(2)] for b in range(B)]
-        d_scales = [[kept([P, 512], U8, "ds%d%d" % (b, g)) for g in range(2)] for b in range(B)]
+        def copy(engine, out, in_):
+            if engine == SCALAR:
+                nc.scalar.copy(out=out, in_=in_)
+            else:
+                nc.vector.tensor_copy(out=out, in_=in_)
+
+        rope = kept([P, B * 1024], BF16, "rope")[:].rearrange("p (b c n) -> p b c n", b=B, c=2)
+        sin_raw = kept([P, B, 4, 2, 64], BF16, "sin_raw")
+        g_first = work.tile([P, 4, 512], BF16, name="g_first", tag="four_heads", bufs=2)
+        g_k = [work.tile([P, 4, 512], BF16, name="g_k0", tag="four_heads", bufs=2)]
+        g_q = [kept([P, 4, 512], BF16, "g_q0"),
+               kept([P, 4096], BF16, "g_q1")[:].rearrange("p (h n) -> p h n", h=8)]
+        dq = [kept([P, 4 * 512], BF16, "dq0")[:].rearrange("p (j f) -> p j f", j=4),
+              kept([P, 4 * 1024], BF16, "dq1")[:].rearrange("p (j f) -> p j f", j=4)]
+        operands = [("w", s) for s in range(4)] + [("x", b) for b in range(B)]
+        sources = {("w", Q_LO): q_w[0:PASS, :], ("w", Q_HI): q_w[PASS:2 * PASS, :], ("w", V_PASS): v_w,
+                   ("w", K_PASS): k_w, ("x", 0): hidden_states[0], ("x", 1): hidden_states[1]}
+        codes = {op: kept([P, H], U32, "codes_%s%d" % op) for op in operands}
+        scales = {op: kept([P, H], U8, "scales_%s%d" % op) for op in operands}
+        stage_tag = {("w", Q_LO): "a", ("w", K_PASS): "a", ("x", 0): "a",
+                     ("w", Q_HI): "b", ("x", 1): "b", ("w", V_PASS): "c"}
+        d_codes = [[kept([P, PASS], U32, "d_codes%d%d" % (b, g)) for g in range(2)] for b in range(B)]
+        d_scales = [[kept([P, PASS], U8, "d_scales%d%d" % (b, g)) for g in range(2)] for b in range(B)]
         ident = kept([P, P], F32, "ident")
+        raw, staged, g_v, rope_psum, prods, q_prods, z, z_codes, z_scales, d_in, sums = [{} for n in range(11)]
 
-        def heads(grad, b, h0):
-            return grad[b, h0:h0 + 4].rearrange("h (p j) d -> p h (j d)", j=4)
+        turn_tags = ["turn0", "turn1", "turn2"]
+        sum_tags = ["sum0", "sum1", "sum2", "rope0"]
 
-        def load_v(b, j):
-            g_v[b, j] = work.tile([P, 512], BF16, name="gv", tag="gv", bufs=6)
-            nc.sync.dma_start(out=g_v[b, j][:].rearrange("p (h d) -> p h d", h=4),
-                              in_=grad_2[b].rearrange("h (p j) d -> p j h d", j=4)[:, j])
+        def next_bank(tags, shape):
+            tags[:] = tags[1:] + tags[:1]
+            return psum.tile(shape, F32, name="bank", tag=tags[-1])
 
-        def load_k1():
-            g_k.append(work.tile([P, 4, 512], BF16, name="gk1", tag="g4", bufs=2))
-            nc.sync.dma_start(out=g_k[1][:], in_=heads(grad_1, 1, 0))
+        def load_heads(dst, grad, b, h0):
+            nc.sync.dma_start(out=dst, in_=grad[b, h0:h0 + 4].rearrange("h (p j) d -> p h (j d)", j=4))
 
-        def load_q1():
-            nc.sync.dma_start(out=g_q[1][:, 0:4, :], in_=heads(grad_0, 1, 0))
-            nc.sync.dma_start(out=g_q[1][:, 4:8, :], in_=heads(grad_0, 1, 4))
+        def load_v(r):
+            g_v[r] = work.tile([P, PASS], BF16, name="g_v", tag="g_v", bufs=6)
+            nc.sync.dma_start(out=g_v[r][:].rearrange("p (h d) -> p h d", h=4),
+                              in_=grad_2[r // 4].rearrange("h (p j) d -> p j h d", j=4)[:, r % 4])
 
-        def load_tables():
-            nc.sync.dma_start(out=tab[:, :, 0, :], in_=cos.rearrange("b (p j) d -> p b (j d)", j=4))
-            nc.sync.dma_start(out=sin_raw[:].rearrange("p (b j) a i -> p b (j a i)", b=B), in_=sin.rearrange("b (p j) d -> p b (j d)", j=4))
-
-        w_rows = [q_w[0:512, :], q_w[512:1024, :], v_w, k_w]
-
-        def load_w(s):
-            nc.sync.dma_start(out=w_raw[s][:], in_=w_rows[s].rearrange("(p j) h -> p j h", j=4))
-
-        def load_x(b):
-            x_raw.append(work.tile([P, 4, H], BF16, name="xraw%d" % b, tag="raw", bufs=4))
-            nc.sync.dma_start(out=x_raw[b][:], in_=hidden_states[b].rearrange("(p j) h -> p j h", j=4))
-
-        load_tables()
-        load_w(0)
-        nc.sync.dma_start(out=g_a[:], in_=heads(grad_0, 0, 0))
-        load_w(1)
-        load_w(3)
-        nc.sync.dma_start(out=g_q[0][:], in_=heads(grad_0, 0, 4))
-        nc.sync.dma_start(out=g_k[0][:], in_=heads(grad_1, 0, 0))
-        load_v(0, 0)
-        load_w(2)
-        load_v(0, 1)
-        load_v(0, 2)
-        load_v(0, 3)
-        make_identity(nc, ident[:])
-
-        def turn_bank():
-            st["turns"] = st.get("turns", 0) + 1
-            return psum.tile([P, 4, P], F32, name="turn", tag="turn%d" % (st["turns"] % 3), bufs=1)
-
-        def sum_bank():
-            tags = st["sum_tags"]
-            st["sums"] = st.get("sums", 0) + 1
-            return psum.tile([P, 512], F32, name="sums", tag=tags[st["sums"] % len(tags)], bufs=1)
-
-        st = {}
-
-        def negate():
-            dst = tab[:, :, 1, :].rearrange("p b (j a i) -> p b j a i", j=4, a=2)
-            src = sin_raw[:].rearrange("p (b j) a i -> p b j a i", b=B)
-            nc.vector.tensor_copy(out=dst[:, :, :, 0, :], in_=src[:, :, :, 1, :])
-            nc.vector.tensor_scalar(out=dst[:, :, :, 1, :], in0=src[:, :, :, 0, :], scalar1=-1.0, scalar2=None, op0=MULT)
-
-        def table_turn(b):
-            bank = turn_bank()
-            words = tab[:, b].rearrange("p s c -> p (s c)").bitcast(F32)
-            for c in range(4):
-                nc.tensor.transpose(bank[:, c, :], words[:, c * P:(c + 1) * P], ident[:])
-            turned = work.tile([P, 4, P], F32, name="tabT", tag="t1", bufs=3)
-            nc.scalar.copy(out=turned[:], in_=bank[:])
-            st["tabT", b] = turned
-
-        def table_back(b):
-            bank = psum.tile([P, 4, P], F32, name="table", tag="table%d" % b, bufs=1)
-            for c in range(4):
-                nc.tensor.transpose(bank[:, c, :], st["tabT", b][:, c, :], ident[:])
-            st["table", b] = bank[:].rearrange("p c w -> p (c w)").bitcast(BF16)
-
-        def products(b, s, j, from_sbuf=False):
-            g = g_a[:] if s == 0 else g_k[b][:]
-            table = tab[:, b].rearrange("p s c -> p (s c)") if from_sbuf else st["table", b]
-            table = table.rearrange("p (s j m t) -> p s j t m", s=2, j=4, t=4)
-            gv = g.rearrange("p h (j m t) -> p j t h m", j=4, t=4)[:, j]
-            t1 = work.tile([P, 4, 4, 32], F32, name="t1", tag="t1", bufs=3)
-            t2 = work.tile([P, 4, 4, 32], F32, name="t2", tag="t2", bufs=3)
-            nc.vector.tensor_tensor(out=t1[:], in0=gv, in1=table[:, 0, j].unsqueeze(2).to_broadcast([P, 4, 4, 32]), op=MULT)
-            for half in range(2):
-                src = slice(16 * (1 - half), 16 * (2 - half))
-                dst = slice(16 * half, 16 * (half + 1))
-                nc.vector.tensor_tensor(out=t2[:, :, :, dst], in0=gv[:, :, :, src],
-                                        in1=table[:, 1, j, :, dst].unsqueeze(2).to_broadcast([P, 4, 4, 16]), op=MULT)
-            st["t", b, s, j] = (t1, t2)
-
-        def products_q(b, j, part):
-            nh = g_q[b].shape[1]
-            table = st["table", b].rearrange("p (s j a i) -> p s j a i", s=2, j=4, a=2)
-            gv = g_q[b][:].rearrange("p h (j a i) -> p j h a i", j=4, a=2)[:, j]
-            u = work.tile([P, nh, 2, 64], F32, name="u%d" % part, tag="u%d" % part, bufs=2)
-            nc.vector.tensor_tensor(out=u[:], in0=gv[:, :, ::-1, :] if part else gv,
-                                    in1=table[:, part, j].unsqueeze(1).to_broadcast([P, nh, 2, 64]), op=MULT)
-            st["u", b, j, part] = u
-
-        def add_q(b, j):
-            if j == 0:
-                st["dq", b] = kept([P, 4 * P * g_q[b].shape[1]], BF16, "dq%d" % b)[:].rearrange("p (j c) -> p j c", j=4)
-            nc.gpsimd.tensor_tensor(out=st["dq", b][:, j, :], in0=st["u", b, j, 0][:].rearrange("p h a i -> p (h a i)"),
-                                    in1=st["u", b, j, 1][:].rearrange("p h a i -> p (h a i)"), op=ADD)
-
-        def turn_words(b, j, s0, s1, engine):
-            bank = turn_bank()
-            for s in range(s0, s1):
-                src = g_v[b, j][:] if s == 2 else st["dq", b][:, j, 512 * (s - 1 + b):512 * (s + b)]
-                for u in range(2):
-                    nc.tensor.transpose(bank[:, 2 * (s - s0) + u, :], src.bitcast(F32)[:, u:256:2], ident[:])
-            z = z_tile(b, j)
-            dst = z[:, s0:s1, :].bitcast(F32).rearrange("p s (c u) -> p s c u", u=2)
-            src = bank[:, 0:2 * (s1 - s0), :].rearrange("p (s u) c -> p s c u", u=2)
-            if engine == "scalar":
-                nc.scalar.copy(out=dst, in_=src)
-            else:
-                nc.vector.tensor_copy(out=dst, in_=src)
-
-        def d_interleave(b, g, engine, c0, c1):
-            if c0 == 0:
-                st["d", b, g] = work.tile([P, 512, 4], BF16, name="d", tag="d", bufs=3, align_bytes=64)
-            off = 512 * (g - 1 + b)
-            weave(engine, st["d", b, g][:, c0:c1, :], st["dq", b][:, :, off + c0:off + c1])
-
-        def z_tile(b, j):
-            if ("z", b, j) not in st:
-                z = work.tile([P, 2048], BF16, name="z%d%d" % (b, j), tag="z", bufs=6, align_bytes=64)
-                st["z", b, j] = z[:].rearrange("p (s c) -> p s c", s=4)
-                st["zc", b, j] = work.tile([P, 4, P], U32, name="zc", tag="zc", bufs=4, align_bytes=64)
-                st["zs", b, j] = work.tile([P, 4, P], U8, name="zs", tag="zs", bufs=4, align_bytes=64)
-            return st["z", b, j]
-
-        def turn_sum(b, j, s):
-            t1, t2 = st["t", b, s, j]
-            bank = turn_bank()
-            for t in range(4):
-                for n, src in enumerate((t1, t2)):
-                    nc.tensor.matmul(bank[:, t, :], lhsT=src[:].rearrange("p t h m -> p t (h m)")[:, t, :], rhs=ident[:],
-                                     start=(n == 0), stop=(n == 1), is_transpose=True)
-            z = z_tile(b, j)
-            nc.scalar.copy(out=z[:, s, :].rearrange("p (c t) -> p c t", t=4), in_=bank[:].rearrange("p t c -> p c t"))
-
-        def quant_z(b, j, s0, s1):
-            nc.vector.quantize_mx(out=st["zc", b, j][:, s0:s1, :].rearrange("p s c -> p (s c)").bitcast(E5),
-                                  scales=st["zs", b, j][:, s0:s1, :].rearrange("p s c -> p (s c)"),
-                                  in_=st["z", b, j][:, s0:s1, :].rearrange("p s c -> p (s c)"))
-
-        def turn_back(b, u, engine):
-            if u == 0:
-                st["d", b, 0] = work.tile([P, 512, 4], BF16, name="d", tag="d", bufs=3, align_bytes=64)
-            bank = turn_bank()
-            for j in range(4):
-                nc.tensor.transpose(bank[:, j, :], st["z", b, j][:, 0, :].bitcast(F32)[:, u:256:2], ident[:])
-            dst = st["d", b, 0][:].rearrange("p (q u e) j -> p u q e j", u=2, e=2)[:, u]
-            src = bank[:].rearrange("p j q -> p (j q)").bitcast(BF16).rearrange("p (j q e) -> p q e j", j=4, e=2)
-            if engine == "scalar":
-                nc.scalar.copy(out=dst, in_=src)
-            else:
-                nc.vector.tensor_copy(out=dst, in_=src)
-
-        def quant_d(b, g, c0=0, c1=512):
-            nc.vector.quantize_mx(out=d_codes[b][g][:, c0:c1].bitcast(E5), scales=d_scales[b][g][:, c0:c1],
-                                  in_=st["d", b, g][:, c0:c1, :].rearrange("p c j -> p (c j)"))
+        def load_operand(op):
+            raw[op] = work.tile([P, 4, H], BF16, name="raw", tag="raw", bufs=4)
+            nc.sync.dma_start(out=raw[op][:], in_=sources[op].rearrange("(p t) h -> p t h", t=4))
 
         def weave(engine, dst, src):
-            dst = dst.rearrange("p (c i) j -> p c j i", i=4)
-            src = src.rearrange("p j (c i) -> p c j i", i=4)
-            if engine == "scalar":
-                nc.scalar.copy(out=dst, in_=src)
+            copy(engine, dst.rearrange("p (c i) t -> p c t i", i=4), src.rearrange("p t (c i) -> p c t i", i=4))
+
+        def interleave(op, engine, c0, c1):
+            if op not in staged:
+                staged[op] = work.tile([P, H, 4], BF16, name="staged", tag=stage_tag[op], align_bytes=64)
+            dst, src = staged[op][:, c0:c1, :], raw[op][:, :, c0:c1]
+            if engine == GPSIMD:
+                nc.gpsimd.tensor_scalar(out=dst, in0=src.rearrange("p t c -> p c t"), scalar1=1.0, scalar2=0.0,
+                                        op0=MULT, op1=ADD)
             else:
-                nc.vector.tensor_copy(out=dst, in_=src)
+                weave(engine, dst, src)
 
-        def interleave(key, raw, share, slot):
-            engine, c0, c1 = share
-            stage = work.tile([P, c1 - c0, 4], BF16, name="il" + slot, tag="il" + slot,
-                              bufs={"gpsimd": 1, "head": 1, "late": 3, "scalar": 5, "vector": 1}[slot], align_bytes=64)
-            src = raw[:, :, c0:c1].rearrange("p j c -> p c j")
-            if engine == "gpsimd":
-                nc.gpsimd.tensor_scalar(out=stage[:], in0=src, scalar1=1.0, scalar2=0.0, op0=MULT, op1=ADD)
+        def quantise_operand(op):
+            nc.vector.quantize_mx(out=codes[op][:].bitcast(E4M3), scales=scales[op][:],
+                                  in_=staged[op][:].rearrange("p c t -> p (c t)"))
+
+        def rope_into_psum():
+            table = rope[:, :, 1, :].rearrange("p b (j a i) -> p b j a i", j=4, a=2)
+            nc.vector.tensor_copy(out=table[:, :, :, 0, :], in_=sin_raw[:, :, :, 1, :])
+            nc.vector.tensor_scalar(out=table[:, :, :, 1, :], in0=sin_raw[:, :, :, 0, :], scalar1=-1.0, scalar2=None,
+                                    op0=MULT)
+            turned = []
+            for b in range(B):
+                bank = next_bank(turn_tags, [P, 4, P])
+                words = rope[:, b].rearrange("p c n -> p (c n)").bitcast(F32)
+                for n in range(4):
+                    nc.tensor.transpose(bank[:, n, :], words[:, n * P:(n + 1) * P], ident[:])
+                once = work.tile([P, 4, P], F32, name="rope_turned", tag="prod_cos", bufs=3)
+                nc.scalar.copy(out=once[:], in_=bank[:])
+                turned.append(once)
+            for b in range(B):
+                bank = psum.tile([P, 4, P], F32, name="rope_bank", tag="rope%d" % b)
+                for n in range(4):
+                    nc.tensor.transpose(bank[:, n, :], turned[b][:, n, :], ident[:])
+                rope_psum[b] = bank[:].rearrange("p n w -> p (n w)").bitcast(BF16)
+
+        def products_sorted(r, s):
+            b, j = divmod(r, 4)
+            g = g_first if s == Q_LO else g_k[b]
+            g = g[:].rearrange("p h (j m t) -> p j t h m", j=4, t=4)[:, j]
+            table = rope_psum[b].rearrange("p (c j m t) -> p c j t m", c=2, j=4, t=4)
+            by_cos = work.tile([P, 4, 4, 32], F32, name="by_cos", tag="prod_cos", bufs=3)
+            by_sin = work.tile([P, 4, 4, 32], F32, name="by_sin", tag="prod_sin", bufs=3)
+            nc.vector.tensor_tensor(out=by_cos[:], in0=g, in1=table[:, 0, j].unsqueeze(2).to_broadcast([P, 4, 4, 32]),
+                                    op=MULT)
+            for half in range(2):
+                here, other = slice(16 * half, 16 * half + 16), slice(16 - 16 * half, 32 - 16 * half)
+                nc.vector.tensor_tensor(out=by_sin[:, :, :, here], in0=g[:, :, :, other],
+                                        in1=table[:, 1, j, :, here].unsqueeze(2).to_broadcast([P, 4, 4, 16]), op=MULT)
+            prods[r, s] = (by_cos, by_sin)
+
+        def product_q(r, c):
+            b, j = divmod(r, 4)
+            heads = g_q[b].shape[1]
+            g = g_q[b][:].rearrange("p h (j a i) -> p j h a i", j=4, a=2)[:, j]
+            table = rope_psum[b].rearrange("p (c j a i) -> p c j a i", c=2, j=4, a=2)
+            prod = work.tile([P, heads, 2, 64], F32, name="q_prod", tag="q_prod%d" % c, bufs=2)
+            nc.vector.tensor_tensor(out=prod[:], in0=g[:, :, ::-1, :] if c else g,
+                                    in1=table[:, c, j].unsqueeze(1).to_broadcast([P, heads, 2, 64]), op=MULT)
+            q_prods[r, c] = prod[:].rearrange("p h a i -> p (h a i)")
+
+        def add_q(r):
+            nc.gpsimd.tensor_tensor(out=dq[r // 4][:, r % 4, :], in0=q_prods[r, 0], in1=q_prods[r, 1], op=ADD)
+
+        def dq_half(b, g):
+            first = PASS * (g - 1 + b)
+            return dq[b][:, :, first:first + PASS]
+
+        def z_of(r):
+            if r not in z:
+                tile = work.tile([P, 4 * PASS], BF16, name="z", tag="z", bufs=6, align_bytes=64)
+                z[r] = tile[:].rearrange("p (s n) -> p s n", s=4)
+                z_codes[r] = work.tile([P, 4, P], U32, name="z_codes", tag="z_codes", bufs=4, align_bytes=64)
+                z_scales[r] = work.tile([P, 4, P], U8, name="z_scales", tag="z_scales", bufs=4, align_bytes=64)
+            return z[r]
+
+        def turn_sum(r, s):
+            bank = next_bank(turn_tags, [P, 4, P])
+            for t in range(4):
+                for n, prod in enumerate(prods[r, s]):
+                    nc.tensor.matmul(bank[:, t, :], lhsT=prod[:].rearrange("p t h m -> p t (h m)")[:, t, :],
+                                     rhs=ident[:], start=(n == 0), stop=(n == 1), is_transpose=True)
+            nc.scalar.copy(out=z_of(r)[:, s, :].rearrange("p (c t) -> p c t", t=4),
+                           in_=bank[:].rearrange("p t c -> p c t"))
+
+        def turn_words(r, s0, s1):
+            bank = next_bank(turn_tags, [P, 4, P])
+            for s in range(s0, s1):
+                src = g_v[r][:] if s == V_PASS else dq_half(r // 4, s)[:, r % 4, :]
+                for u in range(2):
+                    nc.tensor.transpose(bank[:, 2 * (s - s0) + u, :], src.bitcast(F32)[:, u:2 * P:2], ident[:])
+            nc.scalar.copy(out=z_of(r)[:, s0:s1, :].bitcast(F32).rearrange("p s (c u) -> p s c u", u=2),
+                           in_=bank[:, 0:2 * (s1 - s0), :].rearrange("p (s u) c -> p s c u", u=2))
+
+        def turn_row(r):
+            turn_sum(r, K_PASS)
+            if r < 4:
+                turn_words(r, Q_HI, V_PASS + 1)
             else:
-                weave(engine, stage[:], raw[:, :, c0:c1])
-            st["il", key, c0] = stage
+                turn_words(r, V_PASS, V_PASS + 1)
+                turn_words(r, Q_LO, Q_HI + 1)
 
-        def quant_rows(key, codes, scales, share):
-            engine, c0, c1 = share
-            nc.vector.quantize_mx(out=codes[:, c0:c1].bitcast(E4), scales=scales[:, c0:c1],
-                                  in_=st["il", key, c0][:].rearrange("p c j -> p (c j)"))
+        def quantise_row(r):
+            nc.vector.quantize_mx(out=z_codes[r][:].rearrange("p s c -> p (s c)").bitcast(E5M2),
+                                  scales=z_scales[r][:].rearrange("p s c -> p (s c)"),
+                                  in_=z[r].rearrange("p s n -> p (s n)"))
 
-        def dx_mm(b, j, n, passes):
-            cols = slice(512 * n, 512 * (n + 1))
+        def d_of(b, g):
+            if (b, g) not in d_in:
+                d_in[b, g] = work.tile([P, PASS, 4], BF16, name="d_in", tag="d_in", bufs=3, align_bytes=64)
+            return d_in[b, g]
+
+        def turn_back(u):
+            dst = d_of(0, 0)[:].rearrange("p (n u e) j -> p u n e j", u=2, e=2)[:, u]
+            bank = next_bank(turn_tags, [P, 4, P])
+            for j in range(4):
+                nc.tensor.transpose(bank[:, j, :], z[j][:, Q_LO, :].bitcast(F32)[:, u:2 * P:2], ident[:])
+            pairs = bank[:].rearrange("p j n -> p (j n)").bitcast(BF16)
+            nc.scalar.copy(out=dst, in_=pairs.rearrange("p (j n e) -> p n e j", j=4, e=2))
+
+        def interleave_dq(b, g, engine, c0, c1):
+            weave(engine, d_of(b, g)[:, c0:c1, :], dq_half(b, g)[:, :, c0:c1])
+
+        def quantise_dq(b, g):
+            nc.vector.quantize_mx(out=d_codes[b][g][:].bitcast(E5M2), scales=d_scales[b][g][:],
+                                  in_=d_in[b, g][:].rearrange("p f j -> p (f j)"))
+
+        def dx_passes(r, n, passes):
+            cols = slice(PASS * n, PASS * (n + 1))
             for s in passes:
-                if s == 0:
-                    st["acc", b, j, n] = sum_bank()
-                nc.tensor.matmul_mx(out=st["acc", b, j, n][:], lhsT=st["zc", b, j][:, s, :].bitcast(E5),
-                                    lhsT_scale=st["zs", b, j][:, s, :], rhs=w_codes[s][:, cols].bitcast(E4),
-                                    rhs_scale=w_scales[s][:, cols], start=(s == 0), stop=(s == 2))
+                if s == PASS_ORDER[0]:
+                    sums[r, n] = next_bank(sum_tags, [P, PASS])
+                nc.tensor.matmul_mx(out=sums[r, n][:], lhsT=z_codes[r][:, s, :].bitcast(E5M2),
+                                    lhsT_scale=z_scales[r][:, s, :], rhs=codes["w", s][:, cols].bitcast(E4M3),
+                                    rhs_scale=scales["w", s][:, cols],
+                                    start=(s == PASS_ORDER[0]), stop=(s == PASS_ORDER[-1]))
 
-        def leave(acc, rows, engines=("scalar", "scalar"), halves=False, tag="res"):
-            res = work.tile([P, H], F32, name="res", tag=tag, bufs=4)
+        def dx_row(r):
             for n in range(2):
-                cols = slice(512 * n, 512 * (n + 1))
-                if engines[n] == "scalar":
-                    nc.scalar.copy(out=res[:, cols], in_=acc[n][:])
-                else:
-                    nc.vector.tensor_copy(out=res[:, cols], in_=acc[n][:])
-                if halves:
-                    nc.sync.dma_start(out=rows[:, cols], in_=res[:, cols])
-            if not halves:
-                nc.sync.dma_start(out=rows, in_=res[:])
+                dx_passes(r, n, PASS_ORDER)
 
-        def dx_leave(b, j, engines=("scalar", "scalar")):
-            leave([st["acc", b, j, 0], st["acc", b, j, 1]], out_0[b].rearrange("(p j) h -> p j h", j=4)[:, j, :], engines)
+        def result_tile(tag):
+            return work.tile([P, H], F32, name="result", tag=tag, bufs=4)
+
+        def empty(result, banks, engines, n):
+            copy(engines[n], result[:, PASS * n:PASS * (n + 1)], banks[n][:])
+
+        def leave(banks, rows, engines, tag):
+            result = result_tile(tag)
+            for n in range(2):
+                empty(result, banks, engines, n)
+            nc.sync.dma_start(out=rows, in_=result[:])
+
+        def dx_rows_in_hbm(r):
+            return out_0[r // 4].rearrange("(p j) h -> p j h", j=4)[:, r % 4, :]
+
+        def dx_leave(r, engine=SCALAR):
+            leave([sums[r, 0], sums[r, 1]], dx_rows_in_hbm(r), (engine, engine), "result")
 
         def dw_tile(g, m, engines):
-            acc = [sum_bank(), sum_bank()]
+            banks = [next_bank(sum_tags, [P, PASS]) for n in range(2)]
             rows = slice(P * m, P * (m + 1))
             for n in range(2):
-                cols = slice(512 * n, 512 * (n + 1))
+                cols = slice(PASS * n, PASS * (n + 1))
                 for b in range(B):
-                    nc.tensor.matmul_mx(out=acc[n][:], lhsT=d_codes[b][g][:, rows].bitcast(E5), lhsT_scale=d_scales[b][g][:, rows],
-                                        rhs=x_codes[b][:, cols].bitcast(E4), rhs_scale=x_scales[b][:, cols],
-                                        start=(b == 0), stop=(b == 1))
-            leave(acc, out_1[512 * g + P * m:512 * g + P * (m + 1), :], engines, g == 1 and m == 3, "raw" if g == 0 else "res")
+                    nc.tensor.matmul_mx(out=banks[n][:], lhsT=d_codes[b][g][:, rows].bitcast(E5M2),
+                                        lhsT_scale=d_scales[b][g][:, rows], rhs=codes["x", b][:, cols].bitcast(E4M3),
+                                        rhs_scale=scales["x", b][:, cols], start=(b == 0), stop=(b == B - 1))
+            leave(banks, out_1[PASS * g + P * m:PASS * g + P * (m + 1), :], engines, "raw" if g == 0 else "result")
 
-        def il(op, engine, c0, c1, slot=None):
-            interleave(op, (w_raw if op[0] == "w" else x_raw)[op[1]], (engine, c0, c1), slot or engine)
+        x_done = [0]
 
-        def qr(op, c0, c1):
-            codes, scales = (w_codes, w_scales) if op[0] == "w" else (x_codes, x_scales)
-            quant_rows(op, codes[op[1]], scales[op[1]], (None, c0, c1))
+        def interleave_x(engine, width):
+            b, c0 = divmod(x_done[0], H)
+            interleave(("x", b), engine, c0, c0 + width)
+            x_done[0] = x_done[0] + width
 
-        SV = ("scalar", "vector")
-        SS = ("scalar", "scalar")
-        W0, W1, W2, W3, X0, X1 = ("w", 0), ("w", 1), ("w", 2), ("w", 3), ("x", 0), ("x", 1)
-        G, SC, V = "gpsimd", "scalar", "vector"
-        VS = (V, SC)
-        ALL = (0, 1, 3, 2)
-        def row_products(b, j):
-            products_q(b, j, 0)
-            products_q(b, j, 1)
+        nc.sync.dma_start(out=rope[:, :, 0, :], in_=cos.rearrange("b (p j) d -> p b (j d)", j=4))
+        nc.sync.dma_start(out=sin_raw[:].rearrange("p b j a i -> p b (j a i)"),
+                          in_=sin.rearrange("b (p j) d -> p b (j d)", j=4))
+        load_operand(("w", Q_LO))
+        load_heads(g_first[:], grad_0, 0, 0)
+        load_operand(("w", Q_HI))
+        load_operand(("w", K_PASS))
+        load_heads(g_q[0][:], grad_0, 0, 4)
+        load_heads(g_k[0][:], grad_1, 0, 0)
+        load_v(0)
+        load_operand(("w", V_PASS))
+        for r in range(1, 4):
+            load_v(r)
+        load_heads(g_q[1][:, 0:4, :], grad_0, 1, 0)
+        load_heads(g_q[1][:, 4:8, :], grad_0, 1, 4)
+        make_identity(nc, ident[:])
+        rope_into_psum()
 
-        def row_mm(r):
-            dx_mm(r // 4, r % 4, 0, ALL)
-            dx_mm(r // 4, r % 4, 1, ALL)
+        interleave(("w", Q_LO), GPSIMD, 0, W_GPSIMD)
+        interleave(("w", Q_LO), GPSIMD, W_GPSIMD, W_FIRST_GPSIMD)
+        interleave(("w", Q_LO), SCALAR, W_FIRST_GPSIMD, H)
+        interleave(("w", Q_HI), GPSIMD, 0, W_GPSIMD)
+        interleave(("w", Q_HI), SCALAR, W_GPSIMD, W_CUT)
+        for r in range(4):
+            products_sorted(r, Q_LO)
+            turn_sum(r, Q_LO)
+            if r == 1:
+                interleave(("w", Q_HI), SCALAR, W_CUT, H)
+        g_k.append(work.tile([P, 4, 512], BF16, name="g_k1", tag="four_heads", bufs=2))
+        load_heads(g_k[1][:], grad_1, 1, 0)
+        load_v(4)
+        load_v(5)
+        load_operand(("x", 0))
+        load_operand(("x", 1))
+        quantise_operand(("w", Q_LO))
+        interleave(("w", K_PASS), GPSIMD, 0, W_GPSIMD)
+        interleave(("w", K_PASS), SCALAR, W_GPSIMD, W_CUT)
+        turn_back(0)
+        interleave(("w", K_PASS), SCALAR, W_CUT, H)
 
-        def row_turn(r, engine=SC):
-            turn_sum(r // 4, r % 4, 3)
-            if r < 4:
-                turn_words(0, r, 1, 3, engine)
+        product_q(0, 0)
+        for r in range(4):
+            product_q(r, 1)
+            add_q(r)
+            products_sorted(r, K_PASS)
+            product_q(r + 1, 0)
+            if r == 1:
+                interleave(("w", V_PASS), GPSIMD, 0, W_GPSIMD)
+            if r < 3:
+                turn_row(r)
+            if r == 0:
+                interleave(("w", V_PASS), SCALAR, W_GPSIMD, W_CUT)
+            if r == 1:
+                load_v(6)
+                load_v(7)
+                interleave(("w", V_PASS), SCALAR, W_CUT, H)
+
+        quantise_row(0)
+        for s in PASS_ORDER[1:]:
+            quantise_operand(("w", s))
+        quantise_row(1)
+        turn_back(1)
+        interleave_dq(0, 1, SCALAR, 0, PASS // 2)
+        for s in PASS_ORDER:
+            for n in range(2):
+                dx_passes(0, n, (s,))
+        dx_leave(0)
+        turn_row(3)
+        interleave_x(SCALAR, X_SCALAR)
+        dx_row(1)
+        dx_leave(1)
+
+        for r in range(4, 8):
+            product_q(r, 1)
+            quantise_row(r - 2)
+            add_q(r)
+            products_sorted(r, K_PASS)
+            if r < 7:
+                interleave_x(GPSIMD, X_GPSIMD)
+                product_q(r + 1, 0)
             else:
-                turn_words(1, r % 4, 2, 3, engine)
-                turn_words(1, r % 4, 0, 2, engine)
+                dx_leave(3, VECTOR)
+            turn_row(r)
+            interleave_x(SCALAR, X_SCALAR)
+            dx_row(r - 2)
+            if r == 5:
+                interleave_dq(0, 1, SCALAR, PASS // 2, PASS)
+            else:
+                dx_leave(r - 2)
 
-        def row_leave(r, engines=SS):
-            dx_leave(r // 4, r % 4, engines)
+        interleave_x(VECTOR, B * H - x_done[0])
+        quantise_row(6)
+        interleave_dq(1, 0, VECTOR, 0, PASS)
+        quantise_operand(("x", 0))
+        quantise_dq(0, 0)
+        quantise_dq(1, 0)
+        quantise_operand(("x", 1))
+        dx_row(6)
+        dx_leave(6)
+        quantise_dq(0, 1)
+        interleave_dq(1, 1, VECTOR, 0, PASS)
+        quantise_row(7)
+        quantise_dq(1, 1)
 
-        def row_quant(r):
-            quant_z(r // 4, r % 4, 0, 4)
-
-        THIRDS = ((0, 384), (384, 768), (768, 1024))
-        st["sum_tags"] = ["sum0", "sum1", "sum2", "table0"]
-        negate()
-        table_turn(0)
-        table_turn(1)
-        table_back(0)
-        table_back(1)
-        il(W0, V, 768, 1024, "head")
-        il(W0, SC, 384, 768)
-        qr(W0, 768, 1024)
-        il(W0, G, 0, 384, "head")
-        il(W1, G, 0, 384)
-        il(W1, SC, 384, 768)
-        load_q1()
-        products(0, 0, 0)
-        turn_sum(0, 0, 0)
-        products(0, 0, 1)
-        turn_sum(0, 1, 0)
-        il(W1, SC, 768, 1024)
-        products(0, 0, 2)
-        turn_sum(0, 2, 0)
-        products(0, 0, 3)
-        load_k1()
-        load_v(1, 0)
-        load_v(1, 1)
-        load_x(0)
-        load_x(1)
-        qr(W0, 384, 768)
-        qr(W1, 384, 768)
-        qr(W1, 0, 384)
-        qr(W0, 0, 384)
-        turn_sum(0, 3, 0)
-        il(W3, G, 0, 384, "head")
-        il(W3, SC, 384, 768)
-        turn_back(0, 0, SC)
-        il(W3, SC, 768, 1024)
-        products_q(0, 0, 0)
-        for j in range(4):
-            products_q(0, j, 1)
-            add_q(0, j)
-            products(0, 3, j)
-            products_q((j + 1) // 4, (j + 1) % 4, 0)
-            if j == 1:
-                il(W2, G, 0, 384)
-            if j < 3:
-                row_turn(j)
-            if j == 0:
-                il(W2, SC, 384, 768)
-            if j == 1:
-                load_v(1, 2)
-                load_v(1, 3)
-                il(W2, SC, 768, 1024)
-        row_quant(0)
-        qr(W1, 768, 1024)
-        for op in (W3, W2):
-            for c0, c1 in THIRDS:
-                qr(op, c0, c1)
-        row_quant(1)
-        turn_back(0, 1, SC)
-        d_interleave(0, 1, SC, 0, 256)
-        row_mm(0)
-        row_leave(0)
-        row_turn(3)
-        XS = ((X0, 0, 256), (X0, 256, 512), (X0, 512, 768), (X1, 0, 256), (X1, 256, 512))
-        XG = ((X0, 768, 896), (X0, 896, 1024), (X1, 512, 640))
-        il(XS[0][0], SC, XS[0][1], XS[0][2])
-        row_mm(1)
-        row_leave(1)
-        for j in range(4):
-            r = 4 + j
-            products_q(1, j, 1)
-            row_quant(r - 2)
-            add_q(1, j)
-            products(1, 3, j)
-            if j < 3:
-                il(XG[j][0], G, XG[j][1], XG[j][2], "late")
-                products_q(1, j + 1, 0)
-            row_turn(r)
-            if j < 3:
-                il(XS[1 + j][0], SC, XS[1 + j][1], XS[1 + j][2])
-            row_mm(r - 2)
-            if j == 1:
-                d_interleave(0, 1, SC, 256, 512)
-            row_leave(r - 2)
-        il(XS[4][0], V, XS[4][1], XS[4][2], SC)
-        il(X1, V, 640, 1024)
-        row_quant(6)
-        d_interleave(1, 0, V, 0, 512)
-        for op, c0, c1 in XG + XS[:3]:
-            qr(op, c0, c1)
-        row_quant(7)
-        for op, c0, c1 in XS[3:]:
-            qr(op, c0, c1)
-        qr(X1, 640, 1024)
-        quant_d(1, 0)
-        quant_d(0, 0)
-        row_mm(6)
-        row_leave(6)
-        quant_d(0, 1)
-        d_interleave(1, 1, V, 0, 512)
-        row_mm(7)
-        st["sum_tags"] = ["turn0", "turn1", "turn2", "table1", "sum0", "sum1", "sum2", "table0"]
-        st["sums"] = -1
-        row_leave(7)
-        quant_d(1, 1)
+        sum_tags[:] = ["rope1"] + turn_tags + sum_tags
         for g in range(2):
             for m in range(4):
-                dw_tile(g, m, SV)
+                dw_tile(g, m, (SCALAR, SCALAR) if (g, m) < (0, 2) else (SCALAR, VECTOR))
+
+        dx_row(7)
+        result = result_tile("raw")
+        for n in range(2):
+            empty(result, [sums[7, 0], sums[7, 1]], (SCALAR, VECTOR), n)
+            nc.sync.dma_start(out=dx_rows_in_hbm(7)[:, PASS * n:PASS * (n + 1)], in_=result[:, PASS * n:PASS * (n + 1)])

@@ -38,7 +38,7 @@ def tile_mistralattention_v_kernel(tc, hidden_states, cos, sin, q_w, k_w, v_w, g
         ctx.enter_context(tc.manual_schedule())
 
         def kept(shape, dtype, name):
-            return keep.tile(shape, dtype, name=name, align_bytes=64)
+            return keep.tile(shape, dtype, name=name, align_bytes=256)
 
         def copy(engine, out, in_):
             if engine == SCALAR:
@@ -90,7 +90,7 @@ def tile_mistralattention_v_kernel(tc, hidden_states, cos, sin, q_w, k_w, v_w, g
 
         def interleave(op, engine, c0, c1):
             if op not in staged:
-                staged[op] = work.tile([P, H, 4], BF16, name="staged", tag=stage_tag[op], align_bytes=64)
+                staged[op] = work.tile([P, H, 4], BF16, name="staged", tag=stage_tag[op], align_bytes=256)
             dst, src = staged[op][:, c0:c1, :], raw[op][:, :, c0:c1]
             if engine == GPSIMD:
                 nc.gpsimd.tensor_scalar(out=dst, in0=src.rearrange("p t c -> p c t"), scalar1=1.0, scalar2=0.0,
@@ -98,9 +98,9 @@ def tile_mistralattention_v_kernel(tc, hidden_states, cos, sin, q_w, k_w, v_w, g
             else:
                 weave(engine, dst, src)
 
-        def quantise_operand(op):
-            nc.vector.quantize_mx(out=codes[op][:].bitcast(E4M3), scales=scales[op][:],
-                                  in_=staged[op][:].rearrange("p c t -> p (c t)"))
+        def quantise_operand(op, c0=0, c1=H):
+            nc.vector.quantize_mx(out=codes[op][:, c0:c1].bitcast(E4M3), scales=scales[op][:, c0:c1],
+                                  in_=staged[op][:, c0:c1, :].rearrange("p c t -> p (c t)"))
 
         def rope_into_psum():
             table = rope[:, :, 1, :].rearrange("p b (j a i) -> p b j a i", j=4, a=2)
@@ -156,10 +156,10 @@ def tile_mistralattention_v_kernel(tc, hidden_states, cos, sin, q_w, k_w, v_w, g
 
         def z_of(r):
             if r not in z:
-                tile = work.tile([P, 4 * PASS], BF16, name="z", tag="z", bufs=6, align_bytes=64)
+                tile = work.tile([P, 4 * PASS], BF16, name="z", tag="z", bufs=6, align_bytes=256)
                 z[r] = tile[:].rearrange("p (s n) -> p s n", s=4)
-                z_codes[r] = work.tile([P, 4, P], U32, name="z_codes", tag="z_codes", bufs=4, align_bytes=64)
-                z_scales[r] = work.tile([P, 4, P], U8, name="z_scales", tag="z_scales", bufs=4, align_bytes=64)
+                z_codes[r] = work.tile([P, 4, P], U32, name="z_codes", tag="z_codes", bufs=4, align_bytes=256)
+                z_scales[r] = work.tile([P, 4, P], U8, name="z_scales", tag="z_scales", bufs=4, align_bytes=256)
             return z[r]
 
         def turn_sum(r, s):
@@ -195,7 +195,7 @@ def tile_mistralattention_v_kernel(tc, hidden_states, cos, sin, q_w, k_w, v_w, g
 
         def d_of(b, g):
             if (b, g) not in d_in:
-                d_in[b, g] = work.tile([P, PASS, 4], BF16, name="d_in", tag="d_in", bufs=3, align_bytes=64)
+                d_in[b, g] = work.tile([P, PASS, 4], BF16, name="d_in", tag="d_in", bufs=3, align_bytes=256)
             return d_in[b, g]
 
         def turn_back(u):
@@ -327,10 +327,11 @@ def tile_mistralattention_v_kernel(tc, hidden_states, cos, sin, q_w, k_w, v_w, g
         turn_back(1)
         interleave_dq(0, 1, SCALAR, 0, PASS // 2)
         for s in PASS_ORDER:
+            if s == PASS_ORDER[-1]:
+                turn_row(3)
             for n in range(2):
                 dx_passes(0, n, (s,))
         dx_leave(0)
-        turn_row(3)
         interleave_x(SCALAR, X_SCALAR)
         dx_row(1)
         dx_leave(1)
@@ -359,7 +360,8 @@ def tile_mistralattention_v_kernel(tc, hidden_states, cos, sin, q_w, k_w, v_w, g
         quantise_operand(("x", 0))
         quantise_dq(0, 0)
         quantise_dq(1, 0)
-        quantise_operand(("x", 1))
+        for n in range(2):
+            quantise_operand(("x", 1), PASS * n, PASS * (n + 1))
         dx_row(6)
         dx_leave(6)
         quantise_dq(0, 1)

@@ -46,8 +46,8 @@ def tile_mistralattention_v_kernel(tc, hidden_states, cos, sin, q_w, k_w, v_w, g
             else:
                 nc.vector.tensor_copy(out=out, in_=in_)
 
-        rope = kept([P, B * 1024], BF16, "rope")[:].rearrange("p (b c n) -> p b c n", b=B, c=2)
-        sin_raw = kept([P, B, 4, 2, 64], BF16, "sin_raw")
+        rope = [kept([P, 1024], BF16, "rope%d" % b)[:].rearrange("p (c n) -> p c n", c=2) for b in range(B)]
+        sin_raw = [kept([P, 4, 2, 64], BF16, "sin_raw%d" % b) for b in range(B)]
         g_first = work.tile([P, 4, 512], BF16, name="g_first", tag="four_heads", bufs=2)
         g_k = [work.tile([P, 4, 512], BF16, name="g_k0", tag="four_heads", bufs=2)]
         g_q = [kept([P, 4, 512], BF16, "g_q0"),
@@ -64,7 +64,8 @@ def tile_mistralattention_v_kernel(tc, hidden_states, cos, sin, q_w, k_w, v_w, g
         d_codes = [[kept([P, PASS], U32, "d_codes%d%d" % (b, g)) for g in range(2)] for b in range(B)]
         d_scales = [[kept([P, PASS], U8, "d_scales%d%d" % (b, g)) for g in range(2)] for b in range(B)]
         ident = kept([P, P], F32, "ident")
-        raw, staged, g_v, rope_psum, prods, q_prods, z, z_codes, z_scales, d_in, sums = [{} for n in range(11)]
+        raw, staged, g_v, rope_turned, rope_psum, prods, q_prods = {}, {}, {}, {}, {}, {}, {}
+        z, z_codes, z_scales, d_in, sums = {}, {}, {}, {}, {}
 
         turn_tags = ["turn0", "turn1", "turn2"]
         sum_tags = ["sum0", "sum1", "sum2", "rope0"]
@@ -75,6 +76,11 @@ def tile_mistralattention_v_kernel(tc, hidden_states, cos, sin, q_w, k_w, v_w, g
 
         def load_heads(dst, grad, b, h0):
             nc.sync.dma_start(out=dst, in_=grad[b, h0:h0 + 4].rearrange("h (p j) d -> p h (j d)", j=4))
+
+        def load_rope(b):
+            nc.sync.dma_start(out=rope[b][:, 0, :], in_=cos[b].rearrange("(p j) d -> p (j d)", j=4))
+            nc.sync.dma_start(out=sin_raw[b][:].rearrange("p j a i -> p (j a i)"),
+                              in_=sin[b].rearrange("(p j) d -> p (j d)", j=4))
 
         def load_v(r):
             g_v[r] = work.tile([P, PASS], BF16, name="g_v", tag="g_v", bufs=6)
@@ -102,25 +108,25 @@ def tile_mistralattention_v_kernel(tc, hidden_states, cos, sin, q_w, k_w, v_w, g
             nc.vector.quantize_mx(out=codes[op][:, c0:c1].bitcast(E4M3), scales=scales[op][:, c0:c1],
                                   in_=staged[op][:, c0:c1, :].rearrange("p c t -> p (c t)"))
 
-        def rope_into_psum():
-            table = rope[:, :, 1, :].rearrange("p b (j a i) -> p b j a i", j=4, a=2)
-            nc.vector.tensor_copy(out=table[:, :, :, 0, :], in_=sin_raw[:, :, :, 1, :])
-            nc.vector.tensor_scalar(out=table[:, :, :, 1, :], in0=sin_raw[:, :, :, 0, :], scalar1=-1.0, scalar2=None,
+        def rope_table(b):
+            table = rope[b][:, 1, :].rearrange("p (j a i) -> p j a i", j=4, a=2)
+            nc.vector.tensor_copy(out=table[:, :, 0, :], in_=sin_raw[b][:, :, 1, :])
+            nc.vector.tensor_scalar(out=table[:, :, 1, :], in0=sin_raw[b][:, :, 0, :], scalar1=-1.0, scalar2=None,
                                     op0=MULT)
-            turned = []
-            for b in range(B):
-                bank = next_bank(turn_tags, [P, 4, P])
-                words = rope[:, b].rearrange("p c n -> p (c n)").bitcast(F32)
-                for n in range(4):
-                    nc.tensor.transpose(bank[:, n, :], words[:, n * P:(n + 1) * P], ident[:])
-                once = work.tile([P, 4, P], F32, name="rope_turned", tag="prod_cos", bufs=3)
-                nc.scalar.copy(out=once[:], in_=bank[:])
-                turned.append(once)
-            for b in range(B):
-                bank = psum.tile([P, 4, P], F32, name="rope_bank", tag="rope%d" % b)
-                for n in range(4):
-                    nc.tensor.transpose(bank[:, n, :], turned[b][:, n, :], ident[:])
-                rope_psum[b] = bank[:].rearrange("p n w -> p (n w)").bitcast(BF16)
+
+        def rope_turn(b):
+            bank = next_bank(turn_tags, [P, 4, P])
+            words = rope[b].rearrange("p c n -> p (c n)").bitcast(F32)
+            for n in range(4):
+                nc.tensor.transpose(bank[:, n, :], words[:, n * P:(n + 1) * P], ident[:])
+            rope_turned[b] = work.tile([P, 4, P], F32, name="rope_turned", tag=stage_tag["w", V_PASS], align_bytes=256)
+            nc.scalar.copy(out=rope_turned[b][:], in_=bank[:])
+
+        def rope_back(b):
+            bank = psum.tile([P, 4, P], F32, name="rope_bank", tag="rope%d" % b)
+            for n in range(4):
+                nc.tensor.transpose(bank[:, n, :], rope_turned[b][:, n, :], ident[:])
+            rope_psum[b] = bank[:].rearrange("p n w -> p (n w)").bitcast(BF16)
 
         def products_sorted(r, s):
             b, j = divmod(r, 4)
@@ -188,10 +194,10 @@ def tile_mistralattention_v_kernel(tc, hidden_states, cos, sin, q_w, k_w, v_w, g
                 turn_words(r, V_PASS, V_PASS + 1)
                 turn_words(r, Q_LO, Q_HI + 1)
 
-        def quantise_row(r):
-            nc.vector.quantize_mx(out=z_codes[r][:].rearrange("p s c -> p (s c)").bitcast(E5M2),
-                                  scales=z_scales[r][:].rearrange("p s c -> p (s c)"),
-                                  in_=z[r].rearrange("p s n -> p (s n)"))
+        def quantise_row(r, s0=0, s1=4):
+            nc.vector.quantize_mx(out=z_codes[r][:, s0:s1, :].rearrange("p s c -> p (s c)").bitcast(E5M2),
+                                  scales=z_scales[r][:, s0:s1, :].rearrange("p s c -> p (s c)"),
+                                  in_=z[r][:, s0:s1, :].rearrange("p s n -> p (s n)"))
 
         def d_of(b, g):
             if (b, g) not in d_in:
@@ -263,14 +269,13 @@ def tile_mistralattention_v_kernel(tc, hidden_states, cos, sin, q_w, k_w, v_w, g
             interleave(("x", b), engine, c0, c0 + width)
             x_done[0] = x_done[0] + width
 
-        nc.sync.dma_start(out=rope[:, :, 0, :], in_=cos.rearrange("b (p j) d -> p b (j d)", j=4))
-        nc.sync.dma_start(out=sin_raw[:].rearrange("p b j a i -> p b (j a i)"),
-                          in_=sin.rearrange("b (p j) d -> p b (j d)", j=4))
+        load_rope(0)
         load_operand(("w", Q_LO))
         load_heads(g_first[:], grad_0, 0, 0)
         load_operand(("w", Q_HI))
-        load_operand(("w", K_PASS))
+        load_rope(1)
         load_heads(g_q[0][:], grad_0, 0, 4)
+        load_operand(("w", K_PASS))
         load_heads(g_k[0][:], grad_1, 0, 0)
         load_v(0)
         load_operand(("w", V_PASS))
@@ -279,7 +284,9 @@ def tile_mistralattention_v_kernel(tc, hidden_states, cos, sin, q_w, k_w, v_w, g
         load_heads(g_q[1][:, 0:4, :], grad_0, 1, 0)
         load_heads(g_q[1][:, 4:8, :], grad_0, 1, 4)
         make_identity(nc, ident[:])
-        rope_into_psum()
+        rope_table(0)
+        rope_turn(0)
+        rope_back(0)
 
         interleave(("w", Q_LO), GPSIMD, 0, W_GPSIMD)
         interleave(("w", Q_LO), GPSIMD, W_GPSIMD, W_FIRST_GPSIMD)
@@ -297,10 +304,17 @@ def tile_mistralattention_v_kernel(tc, hidden_states, cos, sin, q_w, k_w, v_w, g
         load_v(5)
         load_operand(("x", 0))
         load_operand(("x", 1))
+        rope_table(1)
+        quantise_operand(("w", Q_HI), 0, W_GPSIMD)
+        quantise_operand(("w", Q_HI), W_GPSIMD, W_CUT)
+        for r in range(2):
+            quantise_row(r, Q_LO, Q_LO + 1)
         quantise_operand(("w", Q_LO))
+        rope_turn(1)
         interleave(("w", K_PASS), GPSIMD, 0, W_GPSIMD)
         interleave(("w", K_PASS), SCALAR, W_GPSIMD, W_CUT)
         turn_back(0)
+        rope_back(1)
         interleave(("w", K_PASS), SCALAR, W_CUT, H)
 
         product_q(0, 0)
@@ -320,20 +334,27 @@ def tile_mistralattention_v_kernel(tc, hidden_states, cos, sin, q_w, k_w, v_w, g
                 load_v(7)
                 interleave(("w", V_PASS), SCALAR, W_CUT, H)
 
-        quantise_row(0)
-        for s in PASS_ORDER[1:]:
+        quantise_row(0, Q_HI, K_PASS)
+        quantise_row(0, K_PASS, K_PASS + 1)
+        quantise_operand(("w", Q_HI), W_CUT, H)
+        for s in PASS_ORDER[2:]:
             quantise_operand(("w", s))
-        quantise_row(1)
+        quantise_row(1, Q_HI, K_PASS)
+        quantise_row(1, K_PASS, K_PASS + 1)
+        for r in range(2):
+            for n in range(2):
+                dx_passes(r, n, PASS_ORDER[:1])
         turn_back(1)
         interleave_dq(0, 1, SCALAR, 0, PASS // 2)
-        for s in PASS_ORDER:
+        for s in PASS_ORDER[1:]:
             if s == PASS_ORDER[-1]:
                 turn_row(3)
             for n in range(2):
                 dx_passes(0, n, (s,))
         dx_leave(0)
         interleave_x(SCALAR, X_SCALAR)
-        dx_row(1)
+        for n in range(2):
+            dx_passes(1, n, PASS_ORDER[1:])
         dx_leave(1)
 
         for r in range(4, 8):

from contextlib import ExitStack

import concourse.mybir as mybir
from concourse.masks import make_identity

B, H = 2, 1024
FLOPS = 2 * 1024 * 2048 * 1024 + 2 * 1024 * 1024 * 1024

F32 = mybir.dt.float32
BF16 = mybir.dt.bfloat16
U32 = mybir.dt.uint32
U8 = mybir.dt.uint8
E4M3 = mybir.dt.float8_e4m3fn_x4
E5M2 = mybir.dt.float8_e5m2_x4
MULT = mybir.AluOpType.mult
ADD = mybir.AluOpType.add

P = 128
PASS = 512
Q_LO, Q_HI, V_PASS, K_PASS = 0, 1, 2, 3
PASS_ORDER = (Q_LO, Q_HI, K_PASS, V_PASS)
SCALAR, VECTOR, GPSIMD = "scalar", "vector", "gpsimd"

W_GPSIMD = 384
W_CUT = 768
W_FIRST_GPSIMD = 640
X_SCALAR = 256
X_GPSIMD = 128


def tile_mistralattention_v_kernel(tc, hidden_states, cos, sin, q_w, k_w, v_w, grad_0, grad_1, grad_2,
                                                out_0, out_1):
    nc = tc.nc
    with ExitStack() as ctx:
        keep = ctx.enter_context(tc.tile_pool(name="keep", bufs=1))
        work = ctx.enter_context(tc.tile_pool(name="work", bufs=1))
        psum = ctx.enter_context(tc.psum_pool(name="psum", bufs=1))
        ctx.enter_context(tc.manual_schedule())

        def kept(shape, dtype, name):
            return keep.tile(shape, dtype, name=name, align_bytes=256)

        def copy(engine, out, in_):
            if engine == SCALAR:
                nc.scalar.copy(out=out, in_=in_)
            else:
                nc.vector.tensor_copy(out=out, in_=in_)

        rope = [kept([P, 1024], BF16, "rope%d" % b)[:].rearrange("p (c n) -> p c n", c=2) for b in range(B)]
        sin_raw = [kept([P, 4, 2, 64], BF16, "sin_raw%d" % b) for b in range(B)]
        g_first = work.tile([P, 4, 512], BF16, name="g_first", tag="four_heads", bufs=2)
        g_k = [work.tile([P, 4, 512], BF16, name="g_k0", tag="four_heads", bufs=2)]
        g_q = [kept([P, 4, 512], BF16, "g_q0"),
               kept([P, 4096], BF16, "g_q1")[:].rearrange("p (h n) -> p h n", h=8)]
        dq = [kept([P, 4 * 512], BF16, "dq0")[:].rearrange("p (j f) -> p j f", j=4),
              kept([P, 4 * 1024], BF16, "dq1")[:].rearrange("p (j f) -> p j f", j=4)]
        operands = [("w", s) for s in range(4)] + [("x", b) for b in range(B)]
        sources = {("w", Q_LO): q_w[0:PASS, :], ("w", Q_HI): q_w[PASS:2 * PASS, :], ("w", V_PASS): v_w,
                   ("w", K_PASS): k_w, ("x", 0): hidden_states[0], ("x", 1): hidden_states[1]}
        codes = {op: kept([P, H], U32, "codes_%s%d" % op) for op in operands}
        scales = {op: kept([P, H], U8, "scales_%s%d" % op) for op in operands}
        stage_tag = {("w", Q_LO): "a", ("w", K_PASS): "a", ("x", 0): "a",
                     ("w", Q_HI): "b", ("x", 1): "b", ("w", V_PASS): "c"}
        d_codes = [[kept([P, PASS], U32, "d_codes%d%d" % (b, g)) for g in range(2)] for b in range(B)]
        d_scales = [[kept([P, PASS], U8, "d_scales%d%d" % (b, g)) for g in range(2)] for b in range(B)]
        ident = kept([P, P], F32, "ident")
        raw, staged, g_v, rope_turned, rope_psum, prods, q_prods = {}, {}, {}, {}, {}, {}, {}
        z, z_codes, z_scales, d_in, sums = {}, {}, {}, {}, {}

        turn_tags = ["turn0", "turn1", "turn2"]
        sum_tags = ["sum0", "sum1", "sum2", "rope0"]

        def next_bank(tags, shape):
            tags[:] = tags[1:] + tags[:1]
            return psum.tile(shape, F32, name="bank", tag=tags[-1])

        def load_heads(dst, grad, b, h0):
            nc.sync.dma_start(out=dst, in_=grad[b, h0:h0 + 4].rearrange("h (p j) d -> p h (j d)", j=4))

        def load_rope(b):
            nc.sync.dma_start(out=rope[b][:, 0, :], in_=cos[b].rearrange("(p j) d -> p (j d)", j=4))
            nc.sync.dma_start(out=sin_raw[b][:].rearrange("p j a i -> p (j a i)"),
                              in_=sin[b].rearrange("(p j) d -> p (j d)", j=4))

        def load_v(r):
            g_v[r] = work.tile([P, PASS], BF16, name="g_v", tag="g_v", bufs=6)
            nc.sync.dma_start(out=g_v[r][:].rearrange("p (h d) -> p h d", h=4),
                              in_=grad_2[r // 4].rearrange("h (p j) d -> p j h d", j=4)[:, r % 4])

        def load_operand(op):
            raw[op] = work.tile([P, 4, H], BF16, name="raw", tag="raw", bufs=4)
            nc.sync.dma_start(out=raw[op][:], in_=sources[op].rearrange("(p t) h -> p t h", t=4))

        def weave(engine, dst, src):
            copy(engine, dst.rearrange("p (c i) t -> p c t i", i=4), src.rearrange("p t (c i) -> p c t i", i=4))

        def interleave(op, engine, c0, c1):
            if op not in staged:
                staged[op] = work.tile([P, H, 4], BF16, name="staged", tag=stage_tag[op], align_bytes=256)
            dst, src = staged[op][:, c0:c1, :], raw[op][:, :, c0:c1]
            if engine == GPSIMD:
                nc.gpsimd.tensor_scalar(out=dst, in0=src.rearrange("p t c -> p c t"), scalar1=1.0, scalar2=0.0,
                                        op0=MULT, op1=ADD)
            else:
                weave(engine, dst, src)

        def quantise_operand(op, c0=0, c1=H):
            nc.vector.quantize_mx(out=codes[op][:, c0:c1].bitcast(E4M3), scales=scales[op][:, c0:c1],
                                  in_=staged[op][:, c0:c1, :].rearrange("p c t -> p (c t)"))

        def rope_table(b):
            table = rope[b][:, 1, :].rearrange("p (j a i) -> p j a i", j=4, a=2)
            nc.vector.tensor_copy(out=table[:, :, 0, :], in_=sin_raw[b][:, :, 1, :])
            nc.vector.tensor_scalar(out=table[:, :, 1, :], in0=sin_raw[b][:, :, 0, :], scalar1=-1.0, scalar2=None,
                                    op0=MULT)

        def rope_turn(b):
            bank = next_bank(turn_tags, [P, 4, P])
            words = rope[b].rearrange("p c n -> p (c n)").bitcast(F32)
            for n in range(4):
                nc.tensor.transpose(bank[:, n, :], words[:, n * P:(n + 1) * P], ident[:])
            rope_turned[b] = work.tile([P, 4, P], F32, name="rope_turned", tag=stage_tag["w", V_PASS], align_bytes=256)
            nc.scalar.copy(out=rope_turned[b][:], in_=bank[:])

        def rope_back(b):
            bank = psum.tile([P, 4, P], F32, name="rope_bank", tag="rope%d" % b)
            for n in range(4):
                nc.tensor.transpose(bank[:, n, :], rope_turned[b][:, n, :], ident[:])
            rope_psum[b] = bank[:].rearrange("p n w -> p (n w)").bitcast(BF16)

        def products_sorted(r, s):
            b, j = divmod(r, 4)
            g = g_first if s == Q_LO else g_k[b]
            g = g[:].rearrange("p h (j m t) -> p j t h m", j=4, t=4)[:, j]
            table = rope_psum[b].rearrange("p (c j m t) -> p c j t m", c=2, j=4, t=4)
            by_cos = work.tile([P, 4, 4, 32], F32, name="by_cos", tag="prod_cos", bufs=3)
            by_sin = work.tile([P, 4, 4, 32], F32, name="by_sin", tag="prod_sin", bufs=3)
            nc.vector.tensor_tensor(out=by_cos[:], in0=g, in1=table[:, 0, j].unsqueeze(2).to_broadcast([P, 4, 4, 32]),
                                    op=MULT)
            for half in range(2):
                here, other = slice(16 * half, 16 * half + 16), slice(16 - 16 * half, 32 - 16 * half)
                nc.vector.tensor_tensor(out=by_sin[:, :, :, here], in0=g[:, :, :, other],
                                        in1=table[:, 1, j, :, here].unsqueeze(2).to_broadcast([P, 4, 4, 16]), op=MULT)
            prods[r, s] = (by_cos, by_sin)

        def product_q(r, c):
            b, j = divmod(r, 4)
            heads = g_q[b].shape[1]
            g = g_q[b][:].rearrange("p h (j a i) -> p j h a i", j=4, a=2)[:, j]
            table = rope_psum[b].rearrange("p (c j a i) -> p c j a i", c=2, j=4, a=2)
            prod = work.tile([P, heads, 2, 64], F32, name="q_prod", tag="q_prod%d" % c, bufs=2)
            nc.vector.tensor_tensor(out=prod[:], in0=g[:, :, ::-1, :] if c else g,
                                    in1=table[:, c, j].unsqueeze(1).to_broadcast([P, heads, 2, 64]), op=MULT)
            q_prods[r, c] = prod[:].rearrange("p h a i -> p (h a i)")

        def add_q(r):
            nc.gpsimd.tensor_tensor(out=dq[r // 4][:, r % 4, :], in0=q_prods[r, 0], in1=q_prods[r, 1], op=ADD)

        def dq_half(b, g):
            first = PASS * (g - 1 + b)
            return dq[b][:, :, first:first + PASS]

        def z_of(r):
            if r not in z:
                tile = work.tile([P, 4 * PASS], BF16, name="z", tag="z", bufs=6, align_bytes=256)
                z[r] = tile[:].rearrange("p (s n) -> p s n", s=4)
                z_codes[r] = work.tile([P, 4, P], U32, name="z_codes", tag="z_codes", bufs=4, align_bytes=256)
                z_scales[r] = work.tile([P, 4, P], U8, name="z_scales", tag="z_scales", bufs=4, align_bytes=256)
            return z[r]

        def turn_sum(r, s):
            bank = next_bank(turn_tags, [P, 4, P])
            for t in range(4):
                for n, prod in enumerate(prods[r, s]):
                    nc.tensor.matmul(bank[:, t, :], lhsT=prod[:].rearrange("p t h m -> p t (h m)")[:, t, :],
                                     rhs=ident[:], start=(n == 0), stop=(n == 1), is_transpose=True)
            nc.scalar.copy(out=z_of(r)[:, s, :].rearrange("p (c t) -> p c t", t=4),
                           in_=bank[:].rearrange("p t c -> p c t"))

        def turn_words(r, s0, s1):
            bank = next_bank(turn_tags, [P, 4, P])
            for s in range(s0, s1):
                src = g_v[r][:] if s == V_PASS else dq_half(r // 4, s)[:, r % 4, :]
                for u in range(2):
                    nc.tensor.transpose(bank[:, 2 * (s - s0) + u, :], src.bitcast(F32)[:, u:2 * P:2], ident[:])
            nc.scalar.copy(out=z_of(r)[:, s0:s1, :].bitcast(F32).rearrange("p s (c u) -> p s c u", u=2),
                           in_=bank[:, 0:2 * (s1 - s0), :].rearrange("p (s u) c -> p s c u", u=2))

        def turn_row(r):
            turn_sum(r, K_PASS)
            if r < 4:
                turn_words(r, Q_HI, V_PASS + 1)
            else:
                turn_words(r, V_PASS, V_PASS + 1)
                turn_words(r, Q_LO, Q_HI + 1)

        def quantise_row(r, s0=0, s1=4):
            nc.vector.quantize_mx(out=z_codes[r][:, s0:s1, :].rearrange("p s c -> p (s c)").bitcast(E5M2),
                                  scales=z_scales[r][:, s0:s1, :].rearrange("p s c -> p (s c)"),
                                  in_=z[r][:, s0:s1, :].rearrange("p s n -> p (s n)"))

        def d_of(b, g):
            if (b, g) not in d_in:
                d_in[b, g] = work.tile([P, PASS, 4], BF16, name="d_in", tag="d_in", bufs=3, align_bytes=256)
            return d_in[b, g]

        def turn_back(u):
            dst = d_of(0, 0)[:].rearrange("p (n u e) j -> p u n e j", u=2, e=2)[:, u]
            bank = next_bank(turn_tags, [P, 4, P])
            for j in range(4):
                nc.tensor.transpose(bank[:, j, :], z[j][:, Q_LO, :].bitcast(F32)[:, u:2 * P:2], ident[:])
            pairs = bank[:].rearrange("p j n -> p (j n)").bitcast(BF16)
            nc.scalar.copy(out=dst, in_=pairs.rearrange("p (j n e) -> p n e j", j=4, e=2))

        def interleave_dq(b, g, engine, c0, c1):
            weave(engine, d_of(b, g)[:, c0:c1, :], dq_half(b, g)[:, :, c0:c1])

        def quantise_dq(b, g):
            nc.vector.quantize_mx(out=d_codes[b][g][:].bitcast(E5M2), scales=d_scales[b][g][:],
                                  in_=d_in[b, g][:].rearrange("p f j -> p (f j)"))

        def dx_passes(r, n, passes):
            cols = slice(PASS * n, PASS * (n + 1))
            for s in passes:
                if s == PASS_ORDER[0]:
                    sums[r, n] = next_bank(sum_tags, [P, PASS])
                nc.tensor.matmul_mx(out=sums[r, n][:], lhsT=z_codes[r][:, s, :].bitcast(E5M2),
                                    lhsT_scale=z_scales[r][:, s, :], rhs=codes["w", s][:, cols].bitcast(E4M3),
                                    rhs_scale=scales["w", s][:, cols],
                                    start=(s == PASS_ORDER[0]), stop=(s == PASS_ORDER[-1]))

        def dx_row(r):
            for n in range(2):
                dx_passes(r, n, PASS_ORDER)

        def result_tile(tag):
            return work.tile([P, H], F32, name="result", tag=tag, bufs=4)

        def empty(result, banks, engines, n):
            copy(engines[n], result[:, PASS * n:PASS * (n + 1)], banks[n][:])

        def leave(banks, rows, engines, tag):
            result = result_tile(tag)
            for n in range(2):
                empty(result, banks, engines, n)
            nc.sync.dma_start(out=rows, in_=result[:])

        def dx_rows_in_hbm(r):
            return out_0[r // 4].rearrange("(p j) h -> p j h", j=4)[:, r % 4, :]

        def dx_leave(r, engine=SCALAR):
            leave([sums[r, 0], sums[r, 1]], dx_rows_in_hbm(r), (engine, engine), "result")

        def dw_tile(g, m, engines):
            banks = [next_bank(sum_tags, [P, PASS]) for n in range(2)]
            rows = slice(P * m, P * (m + 1))
            for n in range(2):
                cols = slice(PASS * n, PASS * (n + 1))
                for b in range(B):
                    nc.tensor.matmul_mx(out=banks[n][:], lhsT=d_codes[b][g][:, rows].bitcast(E5M2),
                                        lhsT_scale=d_scales[b][g][:, rows], rhs=codes["x", b][:, cols].bitcast(E4M3),
                                        rhs_scale=scales["x", b][:, cols], start=(b == 0), stop=(b == B - 1))
            leave(banks, out_1[PASS * g + P * m:PASS * g + P * (m + 1), :], engines, "raw" if g == 0 else "result")

        x_done = [0]

        def interleave_x(engine, width):
            b, c0 = divmod(x_done[0], H)
            interleave(("x", b), engine, c0, c0 + width)
            x_done[0] = x_done[0] + width

        load_rope(0)
        load_operand(("w", Q_LO))
        load_heads(g_first[:], grad_0, 0, 0)
        load_operand(("w", Q_HI))
        load_rope(1)
        load_heads(g_q[0][:], grad_0, 0, 4)
        load_operand(("w", K_PASS))
        load_heads(g_k[0][:], grad_1, 0, 0)
        load_v(0)
        load_operand(("w", V_PASS))
        for r in range(1, 4):
            load_v(r)
        load_heads(g_q[1][:, 0:4, :], grad_0, 1, 0)
        load_heads(g_q[1][:, 4:8, :], grad_0, 1, 4)
        make_identity(nc, ident[:])
        rope_table(0)
        rope_turn(0)
        rope_back(0)

        interleave(("w", Q_LO), GPSIMD, 0, W_GPSIMD)
        interleave(("w", Q_LO), GPSIMD, W_GPSIMD, W_FIRST_GPSIMD)
        interleave(("w", Q_LO), SCALAR, W_FIRST_GPSIMD, H)
        interleave(("w", Q_HI), GPSIMD, 0, W_GPSIMD)
        interleave(("w", Q_HI), SCALAR, W_GPSIMD, W_CUT)
        for r in range(4):
            products_sorted(r, Q_LO)
            turn_sum(r, Q_LO)
            if r == 1:
                interleave(("w", Q_HI), SCALAR, W_CUT, H)
        g_k.append(work.tile([P, 4, 512], BF16, name="g_k1", tag="four_heads", bufs=2))
        load_heads(g_k[1][:], grad_1, 1, 0)
        load_v(4)
        load_v(5)
        load_operand(("x", 0))
        load_operand(("x", 1))
        rope_table(1)
        quantise_operand(("w", Q_HI), 0, W_GPSIMD)
        quantise_operand(("w", Q_HI), W_GPSIMD, W_CUT)
        for r in range(2):
            quantise_row(r, Q_LO, Q_LO + 1)
        quantise_operand(("w", Q_LO))
        rope_turn(1)
        interleave(("w", K_PASS), GPSIMD, 0, W_GPSIMD)
        interleave(("w", K_PASS), SCALAR, W_GPSIMD, W_CUT)
        turn_back(0)
        rope_back(1)
        interleave(("w", K_PASS), SCALAR, W_CUT, H)

        product_q(0, 0)
        for r in range(4):
            product_q(r, 1)
            add_q(r)
            products_sorted(r, K_PASS)
            product_q(r + 1, 0)
            if r == 1:
                interleave(("w", V_PASS), GPSIMD, 0, W_GPSIMD)
            if r < 3:
                turn_row(r)
            if r == 0:
                interleave(("w", V_PASS), SCALAR, W_GPSIMD, W_CUT)
            if r == 1:
                load_v(6)
                load_v(7)
                interleave(("w", V_PASS), SCALAR, W_CUT, H)

        quantise_row(0, Q_HI, K_PASS)
        quantise_row(0, K_PASS, K_PASS + 1)
        quantise_operand(("w", Q_HI), W_CUT, H)
        for s in PASS_ORDER[2:]:
            quantise_operand(("w", s))
        quantise_row(1, Q_HI, K_PASS)
        quantise_row(1, K_PASS, K_PASS + 1)
        for r in range(2):
            for n in range(2):
                dx_passes(r, n, PASS_ORDER[:1])
        turn_back(1)
        interleave_dq(0, 1, SCALAR, 0, PASS // 2)
        for s in PASS_ORDER[1:]:
            if s == PASS_ORDER[-1]:
                turn_row(3)
            for n in range(2):
                dx_passes(0, n, (s,))
        dx_leave(0)
        interleave_x(SCALAR, X_SCALAR)
        for n in range(2):
            dx_passes(1, n, PASS_ORDER[1:])
        dx_leave(1)

        for r in range(4, 8):
            product_q(r, 1)
            quantise_row(r - 2)
            add_q(r)
            products_sorted(r, K_PASS)
            if r < 7:
                interleave_x(GPSIMD, X_GPSIMD)
                product_q(r + 1, 0)
            else:
                dx_leave(3, VECTOR)
            turn_row(r)
            interleave_x(SCALAR, X_SCALAR)
            dx_row(r - 2)
            if r == 5:
                interleave_dq(0, 1, SCALAR, PASS // 2, PASS)
            else:
                dx_leave(r - 2)

        interleave_x(VECTOR, B * H - x_done[0])
        quantise_row(6)
        interleave_dq(1, 0, VECTOR, 0, PASS)
        quantise_operand(("x", 0))
        quantise_dq(0, 0)
        quantise_dq(1, 0)
        for n in range(2):
            quantise_operand(("x", 1), PASS * n, PASS * (n + 1))
        dx_row(6)
        dx_leave(6)
        quantise_dq(0, 1)
        interleave_dq(1, 1, VECTOR, 0, PASS)
        quantise_row(7)
        quantise_dq(1, 1)

        sum_tags[:] = ["rope1"] + turn_tags + sum_tags
        for g in range(2):
            for m in range(4):
                dw_tile(g, m, (SCALAR, SCALAR) if (g, m) < (0, 2) else (SCALAR, VECTOR))

        dx_row(7)
        result = result_tile("raw")
        for n in range(2):
            empty(result, [sums[7, 0], sums[7, 1]], (SCALAR, VECTOR), n)
            nc.sync.dma_start(out=dx_rows_in_hbm(7)[:, PASS * n:PASS * (n + 1)], in_=result[:, PASS * n:PASS * (n + 1)])
